import numpy as np
import ml_dtypes


def mxq(x, axis, fmt="e4m3"):
    dtype, down = {"e4m3": (ml_dtypes.float8_e4m3fn, 7), "e5m2": (ml_dtypes.float8_e5m2, 14)}[fmt]
    v = np.moveaxis(np.asarray(x, np.float32).astype(ml_dtypes.bfloat16).astype(np.float64), axis, -1)
    blocks = v.reshape(v.shape[:-1] + (-1, 32))
    amax = np.abs(blocks).max(-1, keepdims=True)
    byte = np.maximum(np.where(amax > 0, np.frexp(amax)[1] - 1 + 127, 0) - down, 1)
    scale = np.exp2(byte - 127.0)
    codes = (blocks / scale).astype(np.float32).astype(dtype).astype(np.float64)
    return np.moveaxis((codes * scale).reshape(v.shape), -1, axis)


WIDE = False


def mx_kscale(k):
    if not WIDE:
        return np.ones(k)
    levels = np.array([10, -10, 5, -5, 0])
    a = np.random.permutation(np.resize(levels, k // 512 * 4)).reshape(k // 512, 4)
    idx = np.arange(k)
    return np.exp2(a[idx // 512, idx % 128 // 32])


BF16 = ml_dtypes.bfloat16


def bf(x):
    return np.asarray(x, np.float32).astype(BF16)


def f64(x):
    return np.asarray(x).astype(np.float64)


E2M1 = np.array([0.0, 0.5, 1.0, 1.5, 2.0, 3.0, 4.0, 6.0, -0.0, -0.5, -1.0, -1.5, -2.0, -3.0, -4.0, -6.0])


def pack_weight(w, fmt):
    k, n = w.shape
    w = f64(bf(w)).reshape(k // 32, 32, n)
    amax = np.abs(w).max(1)
    if fmt == "e4m3":
        byte = np.frexp(amax)[1] - 1 + 127 - 7
    else:
        mant, ex = np.frexp(amax / 6.0)
        byte = np.where(mant > 0.5, ex, ex - 1) + 127
    byte = np.clip(np.where(amax > 0, byte, 1), 1, 254)
    scaled = (w * np.exp2(127.0 - byte)[:, None, :]).reshape(k, n).astype(np.float32)
    by_word = np.ascontiguousarray(scaled.reshape(k // 512, 128, 4, n).transpose(0, 1, 3, 2))
    if fmt == "e4m3":
        words = by_word.astype(ml_dtypes.float8_e4m3fn).view(np.uint8)
    else:
        c = by_word.astype(ml_dtypes.float4_e2m1fn).view(np.uint8) & 0xF
        words = c[..., 0::2] | (c[..., 1::2] << 4)
    return np.ascontiguousarray(words), np.ascontiguousarray(byte.astype(np.uint8).reshape(k // 512, 16, n))


def unpack_weight(words, scales, fmt):
    g, p, n, _ = words.shape
    if fmt == "e4m3":
        vals = np.ascontiguousarray(words).view(ml_dtypes.float8_e4m3fn).astype(np.float64)
    else:
        nib = np.empty((g, p, n, 4), np.uint8)
        nib[..., 0::2] = words & 0xF
        nib[..., 1::2] = words >> 4
        vals = E2M1[nib]
    vals = vals * np.repeat(np.exp2(scales.astype(np.float64) - 127.0), 8, axis=1)[..., None]
    return vals.transpose(0, 1, 3, 2).reshape(g * 512, n)

def pack4(w):
    words, scales = pack_weight(w, "e2m1")
    return words.reshape(words.shape[0], 128, -1), scales


def unpack4(words, scales):
    return unpack_weight(words.reshape(words.shape[0], 128, -1, 2), scales, "e2m1")


B, D, E, H, W, SHIFT = 4, 1024, 1024, 16, 16, 5
EPS = 1e-5


def erf(v):
    a = np.clip(v, -6.0, 6.0)
    a2 = 2.0 * a * a
    term = a.copy()
    tot = a.copy()
    for n in range(120):
        term = term * a2 / (2 * n + 3)
        tot = tot + term
    return 2.0 / np.sqrt(np.pi) * np.exp(-a * a) * tot


def gelu(v):
    return 0.5 * v * (1.0 + erf(v / np.sqrt(2.0)))


def conv1x1(x, w, b):
    n, c, hh, ww = x.shape
    y = w @ mxq(x.reshape(n, c, hh * ww), 1, "e4m3")
    return y.reshape(n, -1, hh, ww) + b[None, :, None, None]


def group_norm1(x, gamma, beta):
    m = x.mean(axis=(1, 2, 3), keepdims=True)
    v = x.var(axis=(1, 2, 3), keepdims=True)
    xh = (x - m) / np.sqrt(v + EPS)
    return xh * gamma[None, :, None, None] + beta[None, :, None, None]


def setup_inputs():
    s = mx_kscale(D)
    x = bf(np.random.standard_normal((B, D, H, W)) * s[None, :, None, None])
    w1 = np.random.standard_normal((E, D)) / np.sqrt(D) / s[None, :]
    w1_words, w1_scales = pack4(np.ascontiguousarray(w1.T))
    b1 = bf(np.random.standard_normal(E) * 0.3)
    g1 = bf(1.0 + 0.1 * np.random.standard_normal(E))
    be1 = bf(0.2 * np.random.standard_normal(E))
    return {"x": x,
            "w1_words": w1_words,
            "w1_scales": w1_scales,
            "b1": b1,
            "g1": g1,
            "be1": be1}


def reference(x, w1_words, w1_scales, b1, g1, be1):
    y = conv1x1(f64(x), unpack4(w1_words, w1_scales).T, f64(b1))
    return gelu(group_norm1(y, f64(g1), f64(be1)))

@@ -1,0 +1,244 @@
+from contextlib import ExitStack
+
+import concourse.mybir as mybir
+from concourse.masks import make_identity
+
+F32 = mybir.dt.float32
+BF16 = mybir.dt.bfloat16
+U8 = mybir.dt.uint8
+U32 = mybir.dt.uint32
+I32 = mybir.dt.int32
+FP8X4 = mybir.dt.float8_e4m3fn_x4
+FP4X4 = mybir.dt.float4_e2m1fn_x4
+ALU = mybir.AluOpType
+ACT = mybir.ActivationFunctionType
+
+SAMPLES = 4
+CHANNELS = 1024
+PIXELS = 256
+EPS = 1e-5
+
+P = 128
+PACK = 4
+K_PASS = P * PACK
+PASSES = CHANNELS // K_PASS
+OUT_TILES = CHANNELS // P
+COLS = 128
+PAIR = 2
+BANKS = OUT_TILES // PAIR
+RUN = 4
+
+FLOPS = 2 * SAMPLES * PIXELS * CHANNELS * CHANNELS
+
+
+def tile_axialshift_pa_kernel(tc, x, w1_words, w1_scales, b1, g1, be1, out):
+    nc = tc.nc
+    with ExitStack() as ctx:
+        keep = ctx.enter_context(tc.tile_pool(name="keep", bufs=1))
+        results = ctx.enter_context(tc.tile_pool(name="results", bufs=6))
+        banks = ctx.enter_context(tc.psum_pool(name="banks", bufs=1))
+
+        x_raw = [keep.tile([P, PASSES, PACK, PIXELS], BF16, name="x_raw%d" % n) for n in range(SAMPLES)]
+        w_words = keep.tile([P, PASSES, 2 * CHANNELS], U8, align_bytes=64)
+        w_scales = keep.tile([P, PASSES, CHANNELS], U8, align_bytes=64)
+
+        def load_x(n):
+            nc.sync.dma_start(
+                out=x_raw[n][:],
+                in_=x[n].rearrange("(g p t) h w -> p g t (h w)", g=PASSES, p=P, t=PACK),
+            )
+
+        nc.vector.memset(w_scales[:].bitcast(I32), 0)
+        load_x(0)
+        nc.sync.dma_start(out=w_words[:].bitcast(I32), in_=w1_words.rearrange("g p b -> p g b").bitcast(I32))
+        for r in range(4):
+            nc.sync.dma_start(
+                out=w_scales[r:P:32].bitcast(I32),
+                in_=w1_scales[:, r:16:4, :].rearrange("g q n -> q g n").bitcast(I32),
+            )
+        for n in range(1, SAMPLES):
+            load_x(n)
+
+        warm_in = keep.tile([P, 1], F32)
+        warm_out = keep.tile([P, 1], F32)
+        nc.vector.memset(warm_in[:], 0.0)
+        nc.scalar.activation(out=warm_out[:], in_=warm_in[:], func=ACT.Gelu)
+
+        param_rows = keep.tile([P, P], BF16)
+        identity = keep.tile([P, P], BF16)
+        nc.gpsimd.memset(param_rows[:], 0.0)
+        for r, vector in enumerate((b1, g1, be1)):
+            nc.gpsimd.dma_start(
+                out=param_rows[r * OUT_TILES : (r + 1) * OUT_TILES, :],
+                in_=vector.rearrange("(j p) -> j p", p=P),
+            )
+        make_identity(nc, identity[:])
+        average = keep.tile([P, P], F32)
+        minus_average = keep.tile([P, P], F32)
+        minus_half = keep.tile([P, 1], F32)
+        nc.gpsimd.memset(average[:], 1.0 / P)
+        nc.gpsimd.memset(minus_average[:], -1.0 / P)
+        nc.gpsimd.memset(minus_half[:], -0.5)
+
+        params = keep.tile([P, 3, OUT_TILES], F32)
+        bias = params[:, 0, :]
+        gain = params[:, 1, :]
+        beta = params[:, 2, :]
+        addend = keep.tile([P, OUT_TILES, 2], F32)
+        bias_gain = keep.tile([P, OUT_TILES], F32)
+
+        def prepare_params():
+            param_cols = banks.tile([P, P], BF16, tag="bank7", name="param_cols")
+            nc.tensor.transpose(param_cols[:], param_rows[:], identity[:])
+            nc.vector.tensor_copy(
+                out=params[:].rearrange("p r j -> p (r j)"), in_=param_cols[:, 0 : 3 * OUT_TILES]
+            )
+            nc.vector.memset(addend[:], PIXELS * EPS)
+            nc.vector.tensor_copy(out=addend[:, :, 0], in_=bias)
+            nc.vector.tensor_tensor(out=bias_gain[:], in0=bias, in1=gain, op=ALU.mult)
+
+        x_grouped = [
+            keep.tile([P, PASSES, PIXELS, PACK], BF16, name="x_grouped%d" % n, align_bytes=64)
+            for n in range(SAMPLES)
+        ]
+        x_codes = [keep.tile([P, PASSES, PIXELS], U32, name="x_codes%d" % n, align_bytes=64) for n in range(SAMPLES)]
+        x_scales = [keep.tile([P, PASSES, PIXELS], U8, name="x_scales%d" % n, align_bytes=64) for n in range(SAMPLES)]
+
+        def regroup(copy, n):
+            for g in range(PASSES):
+                copy(
+                    out=x_grouped[n][:, g].rearrange("p (c i) t -> p c t i", i=RUN),
+                    in_=x_raw[n][:, g].rearrange("p t (c i) -> p c t i", i=RUN),
+                )
+
+        def quantise(n):
+            nc.vector.quantize_mx(
+                out=x_codes[n][:].rearrange("p g w -> p (g w)").bitcast(FP8X4),
+                scales=x_scales[n][:].rearrange("p g w -> p (g w)"),
+                in_=x_grouped[n][:].rearrange("p g w t -> p (g w t)"),
+            )
+
+        products = {}
+        stats = [keep.tile([P, OUT_TILES, 3], F32, name="stats%d" % n) for n in range(SAMPLES)]
+        moments = [keep.tile([P, 2], F32, name="moments%d" % n) for n in range(SAMPLES)]
+        totals = {}
+        var_eps = [keep.tile([P, 1], F32, name="var_eps%d" % n) for n in range(SAMPLES)]
+        rstd = [keep.tile([P, 1], F32, name="rstd%d" % n) for n in range(SAMPLES)]
+        centred = [keep.tile([P, OUT_TILES], F32, name="centred%d" % n) for n in range(SAMPLES)]
+        scale = [keep.tile([P, OUT_TILES], F32, name="scale%d" % n) for n in range(SAMPLES)]
+        shift = [keep.tile([P, OUT_TILES], F32, name="shift%d" % n) for n in range(SAMPLES)]
+
+        def multiply(n, i):
+            product = banks.tile(
+                [P, PAIR, PIXELS], F32, tag="bank%d" % (BANKS * (n % 2) + i), name="product%d_%d" % (n, i)
+            )
+            products[(n, i)] = product
+            for jj in range(PAIR):
+                j = PAIR * i + jj
+                for h in range(PIXELS // COLS):
+                    cols = slice(h * COLS, (h + 1) * COLS)
+                    for g in range(PASSES):
+                        nc.tensor.matmul_mx(
+                            out=product[:, jj, cols],
+                            lhsT=w_words[:, g, 2 * P * j : 2 * P * (j + 1)].bitcast(FP4X4),
+                            lhsT_scale=w_scales[:, g, P * j : P * (j + 1)],
+                            rhs=x_codes[n][:, g, cols].bitcast(FP8X4),
+                            rhs_scale=x_scales[n][:, g, cols],
+                            start=(g == 0),
+                            stop=(g == PASSES - 1),
+                        )
+
+        def statistics(n, i):
+            nc.vector.bn_stats(
+                out=stats[n][:, PAIR * i : PAIR * (i + 1), :].rearrange("p j s -> p (j s)"),
+                in_=products[(n, i)][:].rearrange("p j w -> p w j"),
+            )
+
+        def partition_moments(n):
+            nc.vector.tensor_tensor(out=stats[n][:, :, 1:3], in0=stats[n][:, :, 1:3], in1=addend[:], op=ALU.add)
+            nc.vector.bn_aggr(out=moments[n][:], in_=stats[n][:].rearrange("p j s -> p (j s)"))
+            nc.vector.scalar_tensor_tensor(
+                out=moments[n][:, 1:2],
+                in0=moments[n][:, 0:1],
+                scalar=moments[n][:, 0:1],
+                in1=moments[n][:, 1:2],
+                op0=ALU.mult,
+                op1=ALU.add,
+            )
+
+        def sample_totals(n):
+            total = banks.tile([P, 4], F32, tag="bank%d" % (BANKS * ((n + 1) % 2) + BANKS - 1), name="total%d" % n)
+            totals[n] = total
+            nc.tensor.matmul(out=total[:, 0:2], lhsT=average[:], rhs=moments[n][:], start=True, stop=True)
+            nc.tensor.matmul(out=total[:, 2:4], lhsT=minus_average[:], rhs=moments[n][:], start=True, stop=True)
+
+        def variance(n):
+            total = totals[n]
+            nc.vector.tensor_scalar(
+                out=var_eps[n][:],
+                in0=total[:, 0:1],
+                scalar1=total[:, 2:3],
+                scalar2=total[:, 1:2],
+                op0=ALU.mult,
+                op1=ALU.add,
+            )
+            nc.vector.scalar_tensor_tensor(
+                out=centred[n][:], in0=gain, scalar=total[:, 2:3], in1=bias_gain[:], op0=ALU.mult, op1=ALU.add
+            )
+            nc.gpsimd.tensor_tensor(out=rstd[n][:], in0=var_eps[n][:], in1=minus_half[:], op=ALU.pow)
+
+        def coefficients(n):
+            nc.vector.tensor_scalar(out=scale[n][:], in0=gain, scalar1=rstd[n][:], scalar2=None, op0=ALU.mult)
+            nc.vector.scalar_tensor_tensor(
+                out=shift[n][:], in0=centred[n][:], scalar=rstd[n][:], in1=beta, op0=ALU.mult, op1=ALU.add
+            )
+
+        def gelu_and_store(n, i):
+            result = results.tile([P, PAIR, PIXELS], F32, name="result")
+            for jj in range(PAIR):
+                j = PAIR * i + jj
+                nc.scalar.activation(
+                    out=result[:, jj, :],
+                    in_=products[(n, i)][:, jj, :],
+                    func=ACT.Gelu,
+                    scale=scale[n][:, j : j + 1],
+                    bias=shift[n][:, j : j + 1],
+                )
+            nc.sync.dma_start(
+                out=out[n].rearrange("(j p) h w -> p j (h w)", p=P)[:, PAIR * i : PAIR * (i + 1), :],
+                in_=result[:],
+            )
+
+        regroup(nc.vector.tensor_copy, 0)
+        quantise(0)
+        for n in range(1, SAMPLES):
+            regroup(nc.scalar.copy, n)
+        prepare_params()
+        for i in range(BANKS):
+            multiply(0, i)
+            statistics(0, i)
+            if i == 1:
+                quantise(1)
+        partition_moments(0)
+        for n in range(SAMPLES):
+            following = n + 1
+            if following < SAMPLES:
+                multiply(following, 0)
+                multiply(following, 1)
+            sample_totals(n)
+            if following < SAMPLES:
+                statistics(following, 0)
+            variance(n)
+            if following < SAMPLES:
+                statistics(following, 1)
+            coefficients(n)
+            if following + 1 < SAMPLES:
+                quantise(following + 1)
+            for i in (BANKS - 1, 0, 1, 2):
+                gelu_and_store(n, i)
+            if following < SAMPLES:
+                multiply(following, 2)
+                statistics(following, 2)
+                multiply(following, 3)
+                statistics(following, 3)
+                partition_moments(following)

@@ -27,6 +27,7 @@ COLS = 128
 PAIR = 2
 BANKS = OUT_TILES // PAIR
 RUN = 4
+VECTOR_COPIES = 3
 
 FLOPS = 2 * SAMPLES * PIXELS * CHANNELS * CHANNELS
 
@@ -35,47 +36,58 @@ def tile_axialshift_pa_kernel(tc, x, w1_words, w1_scales, b1, g1, be1, out):
     nc = tc.nc
     with ExitStack() as ctx:
         keep = ctx.enter_context(tc.tile_pool(name="keep", bufs=1))
-        results = ctx.enter_context(tc.tile_pool(name="results", bufs=6))
+        results = ctx.enter_context(tc.tile_pool(name="results", bufs=8))
         banks = ctx.enter_context(tc.psum_pool(name="banks", bufs=1))
+        ctx.enter_context(tc.manual_schedule())
 
         x_raw = [keep.tile([P, PASSES, PACK, PIXELS], BF16, name="x_raw%d" % n) for n in range(SAMPLES)]
         w_words = keep.tile([P, PASSES, 2 * CHANNELS], U8, align_bytes=64)
         w_scales = keep.tile([P, PASSES, CHANNELS], U8, align_bytes=64)
+        param_rows = keep.tile([P, P], BF16)
+        warm_in = keep.tile([P, 1], F32)
+        warm_out = keep.tile([P, 1], F32)
 
         def load_x(n):
+            for g in range(PASSES):
+                nc.sync.dma_start(
+                    out=x_raw[n][:, g],
+                    in_=x[n, g * K_PASS : (g + 1) * K_PASS].rearrange("(p t) h w -> p t (h w)", t=PACK),
+                )
+
+        def load_words(half):
+            columns = slice(half * CHANNELS, (half + 1) * CHANNELS)
             nc.sync.dma_start(
-                out=x_raw[n][:],
-                in_=x[n].rearrange("(g p t) h w -> p g t (h w)", g=PASSES, p=P, t=PACK),
+                out=w_words[:, :, columns].bitcast(I32),
+                in_=w1_words[:, :, columns].rearrange("g p b -> p g b").bitcast(I32),
             )
 
+        nc.vector.memset(param_rows[:], 0.0)
         nc.vector.memset(w_scales[:].bitcast(I32), 0)
+        nc.vector.memset(warm_in[:], 0.0)
+
+        for r, vector in enumerate((b1, g1, be1)):
+            nc.scalar.dma_start(
+                out=param_rows[r * OUT_TILES : (r + 1) * OUT_TILES, :],
+                in_=vector.rearrange("(j p) -> j p", p=P),
+            )
         load_x(0)
-        nc.sync.dma_start(out=w_words[:].bitcast(I32), in_=w1_words.rearrange("g p b -> p g b").bitcast(I32))
+        load_words(0)
         for r in range(4):
             nc.sync.dma_start(
                 out=w_scales[r:P:32].bitcast(I32),
                 in_=w1_scales[:, r:16:4, :].rearrange("g q n -> q g n").bitcast(I32),
             )
+        load_words(1)
         for n in range(1, SAMPLES):
             load_x(n)
 
-        warm_in = keep.tile([P, 1], F32)
-        warm_out = keep.tile([P, 1], F32)
-        nc.vector.memset(warm_in[:], 0.0)
         nc.scalar.activation(out=warm_out[:], in_=warm_in[:], func=ACT.Gelu)
 
-        param_rows = keep.tile([P, P], BF16)
         identity = keep.tile([P, P], BF16)
-        nc.gpsimd.memset(param_rows[:], 0.0)
-        for r, vector in enumerate((b1, g1, be1)):
-            nc.gpsimd.dma_start(
-                out=param_rows[r * OUT_TILES : (r + 1) * OUT_TILES, :],
-                in_=vector.rearrange("(j p) -> j p", p=P),
-            )
-        make_identity(nc, identity[:])
         average = keep.tile([P, P], F32)
         minus_average = keep.tile([P, P], F32)
         minus_half = keep.tile([P, 1], F32)
+        make_identity(nc, identity[:])
         nc.gpsimd.memset(average[:], 1.0 / P)
         nc.gpsimd.memset(minus_average[:], -1.0 / P)
         nc.gpsimd.memset(minus_half[:], -0.5)
@@ -86,10 +98,10 @@ def tile_axialshift_pa_kernel(tc, x, w1_words, w1_scales, b1, g1, be1, out):
         beta = params[:, 2, :]
         addend = keep.tile([P, OUT_TILES, 2], F32)
         bias_gain = keep.tile([P, OUT_TILES], F32)
+        param_cols = banks.tile([P, P], BF16, tag="bank7", name="param_cols")
+        nc.tensor.transpose(param_cols[:], param_rows[:], identity[:])
 
         def prepare_params():
-            param_cols = banks.tile([P, P], BF16, tag="bank7", name="param_cols")
-            nc.tensor.transpose(param_cols[:], param_rows[:], identity[:])
             nc.vector.tensor_copy(
                 out=params[:].rearrange("p r j -> p (r j)"), in_=param_cols[:, 0 : 3 * OUT_TILES]
             )
@@ -104,18 +116,18 @@ def tile_axialshift_pa_kernel(tc, x, w1_words, w1_scales, b1, g1, be1, out):
         x_codes = [keep.tile([P, PASSES, PIXELS], U32, name="x_codes%d" % n, align_bytes=64) for n in range(SAMPLES)]
         x_scales = [keep.tile([P, PASSES, PIXELS], U8, name="x_scales%d" % n, align_bytes=64) for n in range(SAMPLES)]
 
-        def regroup(copy, n):
-            for g in range(PASSES):
-                copy(
-                    out=x_grouped[n][:, g].rearrange("p (c i) t -> p c t i", i=RUN),
-                    in_=x_raw[n][:, g].rearrange("p t (c i) -> p c t i", i=RUN),
-                )
+        def regroup(n, g):
+            copy = nc.vector.tensor_copy if PASSES * n + g < VECTOR_COPIES else nc.scalar.copy
+            copy(
+                out=x_grouped[n][:, g].rearrange("p (c i) t -> p c t i", i=RUN),
+                in_=x_raw[n][:, g].rearrange("p t (c i) -> p c t i", i=RUN),
+            )
 
-        def quantise(n):
+        def quantise(n, g):
             nc.vector.quantize_mx(
-                out=x_codes[n][:].rearrange("p g w -> p (g w)").bitcast(FP8X4),
-                scales=x_scales[n][:].rearrange("p g w -> p (g w)"),
-                in_=x_grouped[n][:].rearrange("p g w t -> p (g w t)"),
+                out=x_codes[n][:, g, :].bitcast(FP8X4),
+                scales=x_scales[n][:, g, :],
+                in_=x_grouped[n][:, g].rearrange("p w t -> p (w t)"),
             )
 
         products = {}
@@ -194,31 +206,33 @@ def tile_axialshift_pa_kernel(tc, x, w1_words, w1_scales, b1, g1, be1, out):
             )
 
         def gelu_and_store(n, i):
-            result = results.tile([P, PAIR, PIXELS], F32, name="result")
             for jj in range(PAIR):
                 j = PAIR * i + jj
+                result = results.tile([P, PIXELS], F32, name="result")
                 nc.scalar.activation(
-                    out=result[:, jj, :],
+                    out=result[:],
                     in_=products[(n, i)][:, jj, :],
                     func=ACT.Gelu,
                     scale=scale[n][:, j : j + 1],
                     bias=shift[n][:, j : j + 1],
                 )
-            nc.sync.dma_start(
-                out=out[n].rearrange("(j p) h w -> p j (h w)", p=P)[:, PAIR * i : PAIR * (i + 1), :],
-                in_=result[:],
-            )
+                nc.sync.dma_start(
+                    out=out[n, j * P : (j + 1) * P].rearrange("p h w -> p (h w)"), in_=result[:]
+                )
 
-        regroup(nc.vector.tensor_copy, 0)
-        quantise(0)
-        for n in range(1, SAMPLES):
-            regroup(nc.scalar.copy, n)
+        for g in range(PASSES):
+            regroup(0, g)
+            quantise(0, g)
         prepare_params()
+        for n in range(1, SAMPLES):
+            for g in range(PASSES):
+                regroup(n, g)
         for i in range(BANKS):
             multiply(0, i)
             statistics(0, i)
             if i == 1:
-                quantise(1)
+                quantise(1, 0)
+                quantise(1, 1)
         partition_moments(0)
         for n in range(SAMPLES):
             following = n + 1
@@ -233,7 +247,8 @@ def tile_axialshift_pa_kernel(tc, x, w1_words, w1_scales, b1, g1, be1, out):
                 statistics(following, 1)
             coefficients(n)
             if following + 1 < SAMPLES:
-                quantise(following + 1)
+                quantise(following + 1, 0)
+                quantise(following + 1, 1)
             for i in (BANKS - 1, 0, 1, 2):
                 gelu_and_store(n, i)
             if following < SAMPLES:

@@ -28,6 +28,7 @@ PAIR = 2
 BANKS = OUT_TILES // PAIR
 RUN = 4
 VECTOR_COPIES = 3
+WARM_UP = 10
 
 FLOPS = 2 * SAMPLES * PIXELS * CHANNELS * CHANNELS
 
@@ -46,6 +47,7 @@ def tile_axialshift_pa_kernel(tc, x, w1_words, w1_scales, b1, g1, be1, out):
         param_rows = keep.tile([P, P], BF16)
         warm_in = keep.tile([P, 1], F32)
         warm_out = keep.tile([P, 1], F32)
+        zeros = keep.tile([P, 4 * P], BF16)
 
         def load_x(n):
             for g in range(PASSES):
@@ -64,6 +66,7 @@ def tile_axialshift_pa_kernel(tc, x, w1_words, w1_scales, b1, g1, be1, out):
         nc.vector.memset(param_rows[:], 0.0)
         nc.vector.memset(w_scales[:].bitcast(I32), 0)
         nc.vector.memset(warm_in[:], 0.0)
+        nc.vector.memset(zeros[:], 0.0)
 
         for r, vector in enumerate((b1, g1, be1)):
             nc.scalar.dma_start(
@@ -98,6 +101,9 @@ def tile_axialshift_pa_kernel(tc, x, w1_words, w1_scales, b1, g1, be1, out):
         beta = params[:, 2, :]
         addend = keep.tile([P, OUT_TILES, 2], F32)
         bias_gain = keep.tile([P, OUT_TILES], F32)
+        for k in range(WARM_UP):
+            scratch = banks.tile([P, 4 * P], F32, tag="bank%d" % (BANKS + k % 3), name="scratch%d" % k)
+            nc.tensor.matmul(out=scratch[:], lhsT=identity[:], rhs=zeros[:], start=True, stop=True)
         param_cols = banks.tile([P, P], BF16, tag="bank7", name="param_cols")
         nc.tensor.transpose(param_cols[:], param_rows[:], identity[:])
 

@@ -212,19 +212,20 @@ def tile_axialshift_pa_kernel(tc, x, w1_words, w1_scales, b1, g1, be1, out):
             )
 
         def gelu_and_store(n, i):
+            result = results.tile([P, PAIR, PIXELS], F32, name="result")
             for jj in range(PAIR):
                 j = PAIR * i + jj
-                result = results.tile([P, PIXELS], F32, name="result")
                 nc.scalar.activation(
-                    out=result[:],
+                    out=result[:, jj, :],
                     in_=products[(n, i)][:, jj, :],
                     func=ACT.Gelu,
                     scale=scale[n][:, j : j + 1],
                     bias=shift[n][:, j : j + 1],
                 )
-                nc.sync.dma_start(
-                    out=out[n, j * P : (j + 1) * P].rearrange("p h w -> p (h w)"), in_=result[:]
-                )
+            nc.sync.dma_start(
+                out=out[n, PAIR * i * P : PAIR * (i + 1) * P].rearrange("(j p) h w -> p j (h w)", p=P),
+                in_=result[:],
+            )
 
         for g in range(PASSES):
             regroup(0, g)

@@ -249,13 +249,14 @@ def tile_axialshift_pa_kernel(tc, x, w1_words, w1_scales, b1, g1, be1, out):
             sample_totals(n)
             if following < SAMPLES:
                 statistics(following, 0)
+            if following + 1 < SAMPLES:
+                quantise(following + 1, 0)
             variance(n)
             if following < SAMPLES:
                 statistics(following, 1)
-            coefficients(n)
             if following + 1 < SAMPLES:
-                quantise(following + 1, 0)
                 quantise(following + 1, 1)
+            coefficients(n)
             for i in (BANKS - 1, 0, 1, 2):
                 gelu_and_store(n, i)
             if following < SAMPLES:

@@ -101,9 +101,17 @@ def tile_axialshift_pa_kernel(tc, x, w1_words, w1_scales, b1, g1, be1, out):
         beta = params[:, 2, :]
         addend = keep.tile([P, OUT_TILES, 2], F32)
         bias_gain = keep.tile([P, OUT_TILES], F32)
-        for k in range(WARM_UP):
-            scratch = banks.tile([P, 4 * P], F32, tag="bank%d" % (BANKS + k % 3), name="scratch%d" % k)
-            nc.tensor.matmul(out=scratch[:], lhsT=identity[:], rhs=zeros[:], start=True, stop=True)
+        warmed = []
+
+        def warm_up(count, moving):
+            for k in range(count):
+                scratch = banks.tile(
+                    [P, 4 * P], F32, tag="bank%d" % (BANKS + len(warmed) % 3), name="scratch%d" % len(warmed)
+                )
+                warmed.append(scratch)
+                nc.tensor.matmul(out=scratch[:], lhsT=identity[:], rhs=moving, start=True, stop=True)
+
+        warm_up(WARM_UP - 6, zeros[:])
         param_cols = banks.tile([P, P], BF16, tag="bank7", name="param_cols")
         nc.tensor.transpose(param_cols[:], param_rows[:], identity[:])
 
@@ -211,7 +219,7 @@ def tile_axialshift_pa_kernel(tc, x, w1_words, w1_scales, b1, g1, be1, out):
                 out=shift[n][:], in0=centred[n][:], scalar=rstd[n][:], in1=beta, op0=ALU.mult, op1=ALU.add
             )
 
-        def gelu_and_store(n, i):
+        def gelu_and_store(n, i, last):
             result = results.tile([P, PAIR, PIXELS], F32, name="result")
             for jj in range(PAIR):
                 j = PAIR * i + jj
@@ -222,14 +230,21 @@ def tile_axialshift_pa_kernel(tc, x, w1_words, w1_scales, b1, g1, be1, out):
                     scale=scale[n][:, j : j + 1],
                     bias=shift[n][:, j : j + 1],
                 )
-            nc.sync.dma_start(
-                out=out[n, PAIR * i * P : PAIR * (i + 1) * P].rearrange("(j p) h w -> p j (h w)", p=P),
-                in_=result[:],
-            )
+                if last:
+                    nc.sync.dma_start(
+                        out=out[n, j * P : (j + 1) * P].rearrange("p h w -> p (h w)"), in_=result[:, jj, :]
+                    )
+            if not last:
+                nc.sync.dma_start(
+                    out=out[n, PAIR * i * P : PAIR * (i + 1) * P].rearrange("(j p) h w -> p j (h w)", p=P),
+                    in_=result[:],
+                )
 
+        warm_up(3, x_raw[0][:, 0].rearrange("p t w -> p (t w)")[:, 0 : 4 * P])
         for g in range(PASSES):
             regroup(0, g)
             quantise(0, g)
+        warm_up(3, x_grouped[0][:, 1].rearrange("p w t -> p (w t)")[:, 0 : 4 * P])
         prepare_params()
         for n in range(1, SAMPLES):
             for g in range(PASSES):
@@ -256,12 +271,17 @@ def tile_axialshift_pa_kernel(tc, x, w1_words, w1_scales, b1, g1, be1, out):
                 statistics(following, 1)
             if following + 1 < SAMPLES:
                 quantise(following + 1, 1)
-            coefficients(n)
-            for i in (BANKS - 1, 0, 1, 2):
-                gelu_and_store(n, i)
-            if following < SAMPLES:
+            early = following == SAMPLES - 1
+            if early:
                 multiply(following, 2)
                 statistics(following, 2)
+            coefficients(n)
+            for i in (BANKS - 1, 0, 1, 2):
+                gelu_and_store(n, i, n == SAMPLES - 1 and i == 2)
+            if following < SAMPLES:
+                if not early:
+                    multiply(following, 2)
+                    statistics(following, 2)
                 multiply(following, 3)
                 statistics(following, 3)
                 partition_moments(following)

@@ -137,11 +137,11 @@ def tile_axialshift_pa_kernel(tc, x, w1_words, w1_scales, b1, g1, be1, out):
                 in_=x_raw[n][:, g].rearrange("p t (c i) -> p c t i", i=RUN),
             )
 
-        def quantise(n, g):
+        def quantise(n):
             nc.vector.quantize_mx(
-                out=x_codes[n][:, g, :].bitcast(FP8X4),
-                scales=x_scales[n][:, g, :],
-                in_=x_grouped[n][:, g].rearrange("p w t -> p (w t)"),
+                out=x_codes[n][:].rearrange("p g w -> p (g w)").bitcast(FP8X4),
+                scales=x_scales[n][:].rearrange("p g w -> p (g w)"),
+                in_=x_grouped[n][:].rearrange("p g w t -> p (g w t)"),
             )
 
         products = {}
@@ -243,8 +243,8 @@ def tile_axialshift_pa_kernel(tc, x, w1_words, w1_scales, b1, g1, be1, out):
         warm_up(3, x_raw[0][:, 0].rearrange("p t w -> p (t w)")[:, 0 : 4 * P])
         for g in range(PASSES):
             regroup(0, g)
-            quantise(0, g)
         warm_up(3, x_grouped[0][:, 1].rearrange("p w t -> p (w t)")[:, 0 : 4 * P])
+        quantise(0)
         prepare_params()
         for n in range(1, SAMPLES):
             for g in range(PASSES):
@@ -253,8 +253,7 @@ def tile_axialshift_pa_kernel(tc, x, w1_words, w1_scales, b1, g1, be1, out):
             multiply(0, i)
             statistics(0, i)
             if i == 1:
-                quantise(1, 0)
-                quantise(1, 1)
+                quantise(1)
         partition_moments(0)
         for n in range(SAMPLES):
             following = n + 1
@@ -264,18 +263,16 @@ def tile_axialshift_pa_kernel(tc, x, w1_words, w1_scales, b1, g1, be1, out):
             sample_totals(n)
             if following < SAMPLES:
                 statistics(following, 0)
-            if following + 1 < SAMPLES:
-                quantise(following + 1, 0)
             variance(n)
             if following < SAMPLES:
                 statistics(following, 1)
-            if following + 1 < SAMPLES:
-                quantise(following + 1, 1)
             early = following == SAMPLES - 1
             if early:
                 multiply(following, 2)
                 statistics(following, 2)
             coefficients(n)
+            if following + 1 < SAMPLES:
+                quantise(following + 1)
             for i in (BANKS - 1, 0, 1, 2):
                 gelu_and_store(n, i, n == SAMPLES - 1 and i == 2)
             if following < SAMPLES:

@@ -155,10 +155,13 @@ def tile_axialshift_pa_kernel(tc, x, w1_words, w1_scales, b1, g1, be1, out):
         shift = [keep.tile([P, OUT_TILES], F32, name="shift%d" % n) for n in range(SAMPLES)]
 
         def multiply(n, i):
-            product = banks.tile(
+            products[(n, i)] = banks.tile(
                 [P, PAIR, PIXELS], F32, tag="bank%d" % (BANKS * (n % 2) + i), name="product%d_%d" % (n, i)
             )
-            products[(n, i)] = product
+            fill(n, i)
+
+        def fill(n, i):
+            product = products[(n, i)]
             for jj in range(PAIR):
                 j = PAIR * i + jj
                 for h in range(PIXELS // COLS):
@@ -282,3 +285,5 @@ def tile_axialshift_pa_kernel(tc, x, w1_words, w1_scales, b1, g1, be1, out):
                 multiply(following, 3)
                 statistics(following, 3)
                 partition_moments(following)
+                if following + 1 < SAMPLES:
+                    fill(following, 0)

@@ -285,5 +285,5 @@ def tile_axialshift_pa_kernel(tc, x, w1_words, w1_scales, b1, g1, be1, out):
                 multiply(following, 3)
                 statistics(following, 3)
                 partition_moments(following)
-                if following + 1 < SAMPLES:
-                    fill(following, 0)
+                fill(following, 0)
+                fill(following, 1)

@@ -88,11 +88,9 @@ def tile_axialshift_pa_kernel(tc, x, w1_words, w1_scales, b1, g1, be1, out):
 
         identity = keep.tile([P, P], BF16)
         average = keep.tile([P, P], F32)
-        minus_average = keep.tile([P, P], F32)
         minus_half = keep.tile([P, 1], F32)
         make_identity(nc, identity[:])
         nc.gpsimd.memset(average[:], 1.0 / P)
-        nc.gpsimd.memset(minus_average[:], -1.0 / P)
         nc.gpsimd.memset(minus_half[:], -0.5)
 
         params = keep.tile([P, 3, OUT_TILES], F32)
@@ -146,7 +144,7 @@ def tile_axialshift_pa_kernel(tc, x, w1_words, w1_scales, b1, g1, be1, out):
 
         products = {}
         stats = [keep.tile([P, OUT_TILES, 3], F32, name="stats%d" % n) for n in range(SAMPLES)]
-        moments = [keep.tile([P, 2], F32, name="moments%d" % n) for n in range(SAMPLES)]
+        moments = [keep.tile([P, 3], F32, name="moments%d" % n) for n in range(SAMPLES)]
         totals = {}
         var_eps = [keep.tile([P, 1], F32, name="var_eps%d" % n) for n in range(SAMPLES)]
         rstd = [keep.tile([P, 1], F32, name="rstd%d" % n) for n in range(SAMPLES)]
@@ -185,7 +183,7 @@ def tile_axialshift_pa_kernel(tc, x, w1_words, w1_scales, b1, g1, be1, out):
 
         def partition_moments(n):
             nc.vector.tensor_tensor(out=stats[n][:, :, 1:3], in0=stats[n][:, :, 1:3], in1=addend[:], op=ALU.add)
-            nc.vector.bn_aggr(out=moments[n][:], in_=stats[n][:].rearrange("p j s -> p (j s)"))
+            nc.vector.bn_aggr(out=moments[n][:, 0:2], in_=stats[n][:].rearrange("p j s -> p (j s)"))
             nc.vector.scalar_tensor_tensor(
                 out=moments[n][:, 1:2],
                 in0=moments[n][:, 0:1],
@@ -194,12 +192,14 @@ def tile_axialshift_pa_kernel(tc, x, w1_words, w1_scales, b1, g1, be1, out):
                 op0=ALU.mult,
                 op1=ALU.add,
             )
+            nc.vector.tensor_scalar(
+                out=moments[n][:, 2:3], in0=moments[n][:, 0:1], scalar1=-1.0, scalar2=None, op0=ALU.mult
+            )
 
         def sample_totals(n):
             total = banks.tile([P, 4], F32, tag="bank%d" % (BANKS * ((n + 1) % 2) + BANKS - 1), name="total%d" % n)
             totals[n] = total
-            nc.tensor.matmul(out=total[:, 0:2], lhsT=average[:], rhs=moments[n][:], start=True, stop=True)
-            nc.tensor.matmul(out=total[:, 2:4], lhsT=minus_average[:], rhs=moments[n][:], start=True, stop=True)
+            nc.tensor.matmul(out=total[:, 0:3], lhsT=average[:], rhs=moments[n][:], start=True, stop=True)
 
         def variance(n):
             total = totals[n]

@@ -28,7 +28,7 @@ PAIR = 2
 BANKS = OUT_TILES // PAIR
 RUN = 4
 VECTOR_COPIES = 3
-WARM_UP = 10
+WARM_UP = 8
 
 FLOPS = 2 * SAMPLES * PIXELS * CHANNELS * CHANNELS
 
@@ -56,35 +56,27 @@ def tile_axialshift_pa_kernel(tc, x, w1_words, w1_scales, b1, g1, be1, out):
                     in_=x[n, g * K_PASS : (g + 1) * K_PASS].rearrange("(p t) h w -> p t (h w)", t=PACK),
                 )
 
-        def load_words(half):
-            columns = slice(half * CHANNELS, (half + 1) * CHANNELS)
-            nc.sync.dma_start(
-                out=w_words[:, :, columns].bitcast(I32),
-                in_=w1_words[:, :, columns].rearrange("g p b -> p g b").bitcast(I32),
-            )
-
-        nc.vector.memset(param_rows[:], 0.0)
         nc.vector.memset(w_scales[:].bitcast(I32), 0)
         nc.vector.memset(warm_in[:], 0.0)
         nc.vector.memset(zeros[:], 0.0)
+        nc.vector.memset(param_rows[:], 0.0)
 
-        for r, vector in enumerate((b1, g1, be1)):
-            nc.scalar.dma_start(
-                out=param_rows[r * OUT_TILES : (r + 1) * OUT_TILES, :],
-                in_=vector.rearrange("(j p) -> j p", p=P),
-            )
         load_x(0)
-        load_words(0)
         for r in range(4):
             nc.sync.dma_start(
                 out=w_scales[r:P:32].bitcast(I32),
                 in_=w1_scales[:, r:16:4, :].rearrange("g q n -> q g n").bitcast(I32),
             )
-        load_words(1)
-        for n in range(1, SAMPLES):
-            load_x(n)
-
+        nc.sync.dma_start(out=w_words[:].bitcast(I32), in_=w1_words.rearrange("g p b -> p g b").bitcast(I32))
+        load_x(1)
         nc.scalar.activation(out=warm_out[:], in_=warm_in[:], func=ACT.Gelu)
+        for r, vector in enumerate((b1, g1, be1)):
+            nc.sync.dma_start(
+                out=param_rows[r * OUT_TILES : (r + 1) * OUT_TILES, :],
+                in_=vector.rearrange("(j p) -> j p", p=P),
+            )
+        for n in range(2, SAMPLES):
+            load_x(n)
 
         identity = keep.tile([P, P], BF16)
         average = keep.tile([P, P], F32)
@@ -99,6 +91,7 @@ def tile_axialshift_pa_kernel(tc, x, w1_words, w1_scales, b1, g1, be1, out):
         beta = params[:, 2, :]
         addend = keep.tile([P, OUT_TILES, 2], F32)
         bias_gain = keep.tile([P, OUT_TILES], F32)
+        nc.vector.memset(addend[:], PIXELS * EPS)
         warmed = []
 
         def warm_up(count, moving):
@@ -109,17 +102,14 @@ def tile_axialshift_pa_kernel(tc, x, w1_words, w1_scales, b1, g1, be1, out):
                 warmed.append(scratch)
                 nc.tensor.matmul(out=scratch[:], lhsT=identity[:], rhs=moving, start=True, stop=True)
 
-        warm_up(WARM_UP - 6, zeros[:])
-        param_cols = banks.tile([P, P], BF16, tag="bank7", name="param_cols")
-        nc.tensor.transpose(param_cols[:], param_rows[:], identity[:])
+        warm_up(WARM_UP - 4, zeros[:])
 
         def prepare_params():
-            nc.vector.tensor_copy(
-                out=params[:].rearrange("p r j -> p (r j)"), in_=param_cols[:, 0 : 3 * OUT_TILES]
-            )
-            nc.vector.memset(addend[:], PIXELS * EPS)
-            nc.vector.tensor_copy(out=addend[:, :, 0], in_=bias)
-            nc.vector.tensor_tensor(out=bias_gain[:], in0=bias, in1=gain, op=ALU.mult)
+            param_cols = banks.tile([P, P], BF16, tag="bank7", name="param_cols")
+            nc.tensor.transpose(param_cols[:], param_rows[:], identity[:])
+            nc.scalar.copy(out=params[:].rearrange("p r j -> p (r j)"), in_=param_cols[:, 0 : 3 * OUT_TILES])
+            nc.gpsimd.tensor_copy(out=addend[:, :, 0], in_=bias)
+            nc.gpsimd.tensor_tensor(out=bias_gain[:], in0=bias, in1=gain, op=ALU.mult)
 
         x_grouped = [
             keep.tile([P, PASSES, PIXELS, PACK], BF16, name="x_grouped%d" % n, align_bytes=64)
@@ -243,20 +233,23 @@ def tile_axialshift_pa_kernel(tc, x, w1_words, w1_scales, b1, g1, be1, out):
                     in_=result[:],
                 )
 
-        warm_up(3, x_raw[0][:, 0].rearrange("p t w -> p (t w)")[:, 0 : 4 * P])
+        warm_up(2, x_raw[0][:, 0].rearrange("p t w -> p (t w)")[:, 0 : 4 * P])
         for g in range(PASSES):
             regroup(0, g)
-        warm_up(3, x_grouped[0][:, 1].rearrange("p w t -> p (w t)")[:, 0 : 4 * P])
+        warm_up(2, x_grouped[0][:, 1].rearrange("p w t -> p (w t)")[:, 0 : 4 * P])
         quantise(0)
-        prepare_params()
-        for n in range(1, SAMPLES):
-            for g in range(PASSES):
-                regroup(n, g)
+        for g in range(PASSES):
+            regroup(1, g)
         for i in range(BANKS):
             multiply(0, i)
             statistics(0, i)
             if i == 1:
                 quantise(1)
+            if i == 2:
+                prepare_params()
+        for n in range(2, SAMPLES):
+            for g in range(PASSES):
+                regroup(n, g)
         partition_moments(0)
         for n in range(SAMPLES):
             following = n + 1

@@ -28,6 +28,7 @@ PAIR = 2
 BANKS = OUT_TILES // PAIR
 RUN = 4
 VECTOR_COPIES = 3
+HELD = SAMPLES - 1
 WARM_UP = 8
 
 FLOPS = 2 * SAMPLES * PIXELS * CHANNELS * CHANNELS
@@ -107,7 +108,7 @@ def tile_axialshift_pa_kernel(tc, x, w1_words, w1_scales, b1, g1, be1, out):
         def prepare_params():
             param_cols = banks.tile([P, P], BF16, tag="bank7", name="param_cols")
             nc.tensor.transpose(param_cols[:], param_rows[:], identity[:])
-            nc.scalar.copy(out=params[:].rearrange("p r j -> p (r j)"), in_=param_cols[:, 0 : 3 * OUT_TILES])
+            nc.vector.tensor_copy(out=params[:].rearrange("p r j -> p (r j)"), in_=param_cols[:, 0 : 3 * OUT_TILES])
             nc.gpsimd.tensor_copy(out=addend[:, :, 0], in_=bias)
             nc.gpsimd.tensor_tensor(out=bias_gain[:], in0=bias, in1=gain, op=ALU.mult)
 
@@ -133,6 +134,7 @@ def tile_axialshift_pa_kernel(tc, x, w1_words, w1_scales, b1, g1, be1, out):
             )
 
         products = {}
+        held = [keep.tile([P, PAIR, PIXELS], F32, name="held%d" % n) for n in range(HELD)]
         stats = [keep.tile([P, OUT_TILES, 3], F32, name="stats%d" % n) for n in range(SAMPLES)]
         moments = [keep.tile([P, 3], F32, name="moments%d" % n) for n in range(SAMPLES)]
         totals = {}
@@ -146,9 +148,6 @@ def tile_axialshift_pa_kernel(tc, x, w1_words, w1_scales, b1, g1, be1, out):
             products[(n, i)] = banks.tile(
                 [P, PAIR, PIXELS], F32, tag="bank%d" % (BANKS * (n % 2) + i), name="product%d_%d" % (n, i)
             )
-            fill(n, i)
-
-        def fill(n, i):
             product = products[(n, i)]
             for jj in range(PAIR):
                 j = PAIR * i + jj
@@ -186,8 +185,12 @@ def tile_axialshift_pa_kernel(tc, x, w1_words, w1_scales, b1, g1, be1, out):
                 out=moments[n][:, 2:3], in0=moments[n][:, 0:1], scalar1=-1.0, scalar2=None, op0=ALU.mult
             )
 
+        def hold(n):
+            nc.scalar.copy(out=held[n][:], in_=products[(n, 0)][:])
+
         def sample_totals(n):
-            total = banks.tile([P, 4], F32, tag="bank%d" % (BANKS * ((n + 1) % 2) + BANKS - 1), name="total%d" % n)
+            bank = BANKS * (n % 2) if n < HELD else BANKS * ((n + 1) % 2) + 1
+            total = banks.tile([P, 4], F32, tag="bank%d" % bank, name="total%d" % n)
             totals[n] = total
             nc.tensor.matmul(out=total[:, 0:3], lhsT=average[:], rhs=moments[n][:], start=True, stop=True)
 
@@ -214,11 +217,12 @@ def tile_axialshift_pa_kernel(tc, x, w1_words, w1_scales, b1, g1, be1, out):
 
         def gelu_and_store(n, i, last):
             result = results.tile([P, PAIR, PIXELS], F32, name="result")
+            source = held[n] if i == 0 and n < HELD else products[(n, i)]
             for jj in range(PAIR):
                 j = PAIR * i + jj
                 nc.scalar.activation(
                     out=result[:, jj, :],
-                    in_=products[(n, i)][:, jj, :],
+                    in_=source[:, jj, :],
                     func=ACT.Gelu,
                     scale=scale[n][:, j : j + 1],
                     bias=shift[n][:, j : j + 1],
@@ -238,45 +242,46 @@ def tile_axialshift_pa_kernel(tc, x, w1_words, w1_scales, b1, g1, be1, out):
             regroup(0, g)
         warm_up(2, x_grouped[0][:, 1].rearrange("p w t -> p (w t)")[:, 0 : 4 * P])
         quantise(0)
-        for g in range(PASSES):
-            regroup(1, g)
+        for n in (1, 2):
+            for g in range(PASSES):
+                regroup(n, g)
         for i in range(BANKS):
             multiply(0, i)
             statistics(0, i)
+            if i == 0:
+                hold(0)
+                for g in range(PASSES):
+                    regroup(3, g)
             if i == 1:
                 quantise(1)
             if i == 2:
                 prepare_params()
-        for n in range(2, SAMPLES):
-            for g in range(PASSES):
-                regroup(n, g)
-        partition_moments(0)
+        multiply(1, 0)
         for n in range(SAMPLES):
             following = n + 1
-            if following < SAMPLES:
-                multiply(following, 0)
+            more = following < SAMPLES
+            partition_moments(n)
+            if more:
                 multiply(following, 1)
             sample_totals(n)
-            if following < SAMPLES:
-                statistics(following, 0)
-            variance(n)
-            if following < SAMPLES:
-                statistics(following, 1)
-            early = following == SAMPLES - 1
-            if early:
+            if more:
                 multiply(following, 2)
+                statistics(following, 0)
+                if following < HELD:
+                    quantise(following + 1)
+                else:
+                    statistics(following, 1)
+            variance(n)
+            if more:
+                multiply(following, 3)
+            if following < HELD:
+                hold(following)
+                multiply(following + 1, 0)
+                statistics(following, 1)
+            if more:
                 statistics(following, 2)
             coefficients(n)
-            if following + 1 < SAMPLES:
-                quantise(following + 1)
-            for i in (BANKS - 1, 0, 1, 2):
-                gelu_and_store(n, i, n == SAMPLES - 1 and i == 2)
-            if following < SAMPLES:
-                if not early:
-                    multiply(following, 2)
-                    statistics(following, 2)
-                multiply(following, 3)
+            for i in (1, 2, 3, 0) if n < HELD else range(BANKS):
+                gelu_and_store(n, i, n == SAMPLES - 1 and i == BANKS - 1)
+            if more:
                 statistics(following, 3)
-                partition_moments(following)
-                fill(following, 0)
-                fill(following, 1)

@@ -148,6 +148,9 @@ def tile_axialshift_pa_kernel(tc, x, w1_words, w1_scales, b1, g1, be1, out):
             products[(n, i)] = banks.tile(
                 [P, PAIR, PIXELS], F32, tag="bank%d" % (BANKS * (n % 2) + i), name="product%d_%d" % (n, i)
             )
+            fill(n, i)
+
+        def fill(n, i):
             product = products[(n, i)]
             for jj in range(PAIR):
                 j = PAIR * i + jj
@@ -267,19 +270,20 @@ def tile_axialshift_pa_kernel(tc, x, w1_words, w1_scales, b1, g1, be1, out):
             if more:
                 multiply(following, 2)
                 statistics(following, 0)
-                if following < HELD:
-                    quantise(following + 1)
-                else:
-                    statistics(following, 1)
+            if following < HELD:
+                quantise(following + 1)
             variance(n)
             if more:
                 multiply(following, 3)
             if following < HELD:
                 hold(following)
                 multiply(following + 1, 0)
-                statistics(following, 1)
             if more:
+                statistics(following, 1)
                 statistics(following, 2)
+            if following < HELD:
+                fill(following, 1)
+                fill(following, 2)
             coefficients(n)
             for i in (1, 2, 3, 0) if n < HELD else range(BANKS):
                 gelu_and_store(n, i, n == SAMPLES - 1 and i == BANKS - 1)

@@ -28,6 +28,8 @@ PAIR = 2
 BANKS = OUT_TILES // PAIR
 RUN = 4
 VECTOR_COPIES = 3
+GROUPS = OUT_TILES + 2
+TERMS = 3
 HELD = SAMPLES - 1
 WARM_UP = 8
 
@@ -86,13 +88,28 @@ def tile_axialshift_pa_kernel(tc, x, w1_words, w1_scales, b1, g1, be1, out):
         nc.gpsimd.memset(average[:], 1.0 / P)
         nc.gpsimd.memset(minus_half[:], -0.5)
 
-        params = keep.tile([P, 3, OUT_TILES], F32)
-        bias = params[:, 0, :]
-        gain = params[:, 1, :]
-        beta = params[:, 2, :]
-        addend = keep.tile([P, OUT_TILES, 2], F32)
+        select = keep.tile([P, 4 * OUT_TILES + SAMPLES * TERMS], BF16)
+        params = keep.tile([P, 4 * OUT_TILES + 2], F32)
+        bias = params[:, 0:OUT_TILES]
+        gain = params[:, OUT_TILES : 2 * OUT_TILES]
+        beta = params[:, 2 * OUT_TILES : 3 * OUT_TILES]
+        cross_weights = params[:, 3 * OUT_TILES : 4 * OUT_TILES + 2]
+        bias_terms = keep.tile([P, SAMPLES, TERMS], F32)
         bias_gain = keep.tile([P, OUT_TILES], F32)
-        nc.vector.memset(addend[:], PIXELS * EPS)
+        squares = keep.tile([P, OUT_TILES], F32)
+        nc.vector.memset(params[:, 4 * OUT_TILES + 1 :], EPS)
+        nc.vector.memset(select[:], 0.0)
+        bias_means = select[0:OUT_TILES, 4 * OUT_TILES :].rearrange("p (n c) -> p n c", c=TERMS)
+        nc.vector.memset(bias_means[:, :, 0], 1.0 / OUT_TILES)
+        nc.vector.memset(bias_means[:, :, 2], -1.0 / OUT_TILES)
+        nc.vector.tensor_copy(out=select[:, 0 : 3 * OUT_TILES], in_=identity[:, 0 : 3 * OUT_TILES])
+        nc.vector.tensor_scalar(
+            out=select[:, 3 * OUT_TILES : 4 * OUT_TILES],
+            in0=identity[:, 0:OUT_TILES],
+            scalar1=0.25,
+            scalar2=None,
+            op0=ALU.mult,
+        )
         warmed = []
 
         def warm_up(count, moving):
@@ -106,11 +123,27 @@ def tile_axialshift_pa_kernel(tc, x, w1_words, w1_scales, b1, g1, be1, out):
         warm_up(WARM_UP - 4, zeros[:])
 
         def prepare_params():
-            param_cols = banks.tile([P, P], BF16, tag="bank7", name="param_cols")
-            nc.tensor.transpose(param_cols[:], param_rows[:], identity[:])
-            nc.vector.tensor_copy(out=params[:].rearrange("p r j -> p (r j)"), in_=param_cols[:, 0 : 3 * OUT_TILES])
-            nc.gpsimd.tensor_copy(out=addend[:, :, 0], in_=bias)
+            columns = banks.tile([P, 4 * P], F32, tag="bank7", name="param_columns")
+            linear = 4 * OUT_TILES
+            nc.tensor.matmul(
+                out=columns[:, 0 : linear + SAMPLES * TERMS], lhsT=param_rows[:], rhs=select[:], start=True, stop=True
+            )
+            nc.vector.tensor_copy(out=params[:, 0:linear], in_=columns[:, 0:linear])
+            nc.vector.tensor_copy(
+                out=bias_terms[:].rearrange("p n c -> p (n c)"), in_=columns[:, linear : linear + SAMPLES * TERMS]
+            )
             nc.gpsimd.tensor_tensor(out=bias_gain[:], in0=bias, in1=gain, op=ALU.mult)
+
+        def square_bias():
+            nc.vector.scalar_tensor_tensor(
+                out=squares[:],
+                in0=bias,
+                scalar=1.0 / OUT_TILES,
+                in1=bias,
+                op0=ALU.mult,
+                op1=ALU.mult,
+                accum_out=params[:, 4 * OUT_TILES : 4 * OUT_TILES + 1],
+            )
 
         x_grouped = [
             keep.tile([P, PASSES, PIXELS, PACK], BF16, name="x_grouped%d" % n, align_bytes=64)
@@ -126,16 +159,19 @@ def tile_axialshift_pa_kernel(tc, x, w1_words, w1_scales, b1, g1, be1, out):
                 in_=x_raw[n][:, g].rearrange("p t (c i) -> p c t i", i=RUN),
             )
 
-        def quantise(n):
+        def quantise(n, passes=slice(0, PASSES)):
             nc.vector.quantize_mx(
-                out=x_codes[n][:].rearrange("p g w -> p (g w)").bitcast(FP8X4),
-                scales=x_scales[n][:].rearrange("p g w -> p (g w)"),
-                in_=x_grouped[n][:].rearrange("p g w t -> p (g w t)"),
+                out=x_codes[n][:, passes].rearrange("p g w -> p (g w)").bitcast(FP8X4),
+                scales=x_scales[n][:, passes].rearrange("p g w -> p (g w)"),
+                in_=x_grouped[n][:, passes].rearrange("p g w t -> p (g w t)"),
             )
 
         products = {}
         held = [keep.tile([P, PAIR, PIXELS], F32, name="held%d" % n) for n in range(HELD)]
-        stats = [keep.tile([P, OUT_TILES, 3], F32, name="stats%d" % n) for n in range(SAMPLES)]
+        stats = [keep.tile([P, GROUPS, 3], F32, name="stats%d" % n) for n in range(SAMPLES)]
+        cross = [keep.tile([P, GROUPS], F32, name="cross%d" % n) for n in range(SAMPLES)]
+        for n in range(SAMPLES):
+            nc.vector.memset(stats[n][:, OUT_TILES:, :], 1.0)
         moments = [keep.tile([P, 3], F32, name="moments%d" % n) for n in range(SAMPLES)]
         totals = {}
         var_eps = [keep.tile([P, 1], F32, name="var_eps%d" % n) for n in range(SAMPLES)]
@@ -174,8 +210,18 @@ def tile_axialshift_pa_kernel(tc, x, w1_words, w1_scales, b1, g1, be1, out):
             )
 
         def partition_moments(n):
-            nc.vector.tensor_tensor(out=stats[n][:, :, 1:3], in0=stats[n][:, :, 1:3], in1=addend[:], op=ALU.add)
-            nc.vector.bn_aggr(out=moments[n][:, 0:2], in_=stats[n][:].rearrange("p j s -> p (j s)"))
+            nc.vector.bn_aggr(
+                out=moments[n][:, 0:2], in_=stats[n][:, 0:OUT_TILES].rearrange("p j s -> p (j s)")
+            )
+            nc.vector.scalar_tensor_tensor(
+                out=cross[n][:],
+                in0=stats[n][:, :, 1],
+                scalar=1.0,
+                in1=cross_weights,
+                op0=ALU.mult,
+                op1=ALU.mult,
+                accum_out=bias_terms[:, n, 1:2],
+            )
             nc.vector.scalar_tensor_tensor(
                 out=moments[n][:, 1:2],
                 in0=moments[n][:, 0:1],
@@ -195,7 +241,11 @@ def tile_axialshift_pa_kernel(tc, x, w1_words, w1_scales, b1, g1, be1, out):
             bank = BANKS * (n % 2) if n < HELD else BANKS * ((n + 1) % 2) + 1
             total = banks.tile([P, 4], F32, tag="bank%d" % bank, name="total%d" % n)
             totals[n] = total
-            nc.tensor.matmul(out=total[:, 0:3], lhsT=average[:], rhs=moments[n][:], start=True, stop=True)
+            terms = (bias_terms[:, n, :], moments[n][:])
+            for k, term in enumerate(terms):
+                nc.tensor.matmul(
+                    out=total[:, 0:TERMS], lhsT=average[:], rhs=term, start=(k == 0), stop=(k == len(terms) - 1)
+                )
 
         def variance(n):
             total = totals[n]
@@ -244,21 +294,25 @@ def tile_axialshift_pa_kernel(tc, x, w1_words, w1_scales, b1, g1, be1, out):
         for g in range(PASSES):
             regroup(0, g)
         warm_up(2, x_grouped[0][:, 1].rearrange("p w t -> p (w t)")[:, 0 : 4 * P])
-        quantise(0)
-        for n in (1, 2):
-            for g in range(PASSES):
-                regroup(n, g)
+        for g in range(PASSES):
+            quantise(0, slice(g, g + 1))
+        regroup(1, 0)
+        quantise(1, slice(0, 1))
+        regroup(1, 1)
+        regroup(2, 0)
         for i in range(BANKS):
             multiply(0, i)
             statistics(0, i)
             if i == 0:
                 hold(0)
+                regroup(2, 1)
                 for g in range(PASSES):
                     regroup(3, g)
             if i == 1:
-                quantise(1)
+                quantise(1, slice(1, 2))
             if i == 2:
                 prepare_params()
+        square_bias()
         multiply(1, 0)
         for n in range(SAMPLES):
             following = n + 1
@@ -283,7 +337,6 @@ def tile_axialshift_pa_kernel(tc, x, w1_words, w1_scales, b1, g1, be1, out):
                 statistics(following, 2)
             if following < HELD:
                 fill(following, 1)
-                fill(following, 2)
             coefficients(n)
             for i in (1, 2, 3, 0) if n < HELD else range(BANKS):
                 gelu_and_store(n, i, n == SAMPLES - 1 and i == BANKS - 1)

@@ -30,7 +30,9 @@ RUN = 4
 VECTOR_COPIES = 3
 GROUPS = OUT_TILES + 2
 TERMS = 3
-HELD = SAMPLES - 1
+HELD = ((0, 0), (1, 0), (1, 1), (2, 0))
+SHARED_COPY = 3
+VECTOR_PIXELS = 96
 WARM_UP = 8
 
 FLOPS = 2 * SAMPLES * PIXELS * CHANNELS * CHANNELS
@@ -153,11 +155,18 @@ def tile_axialshift_pa_kernel(tc, x, w1_words, w1_scales, b1, g1, be1, out):
         x_scales = [keep.tile([P, PASSES, PIXELS], U8, name="x_scales%d" % n, align_bytes=64) for n in range(SAMPLES)]
 
         def regroup(n, g):
-            copy = nc.vector.tensor_copy if PASSES * n + g < VECTOR_COPIES else nc.scalar.copy
-            copy(
-                out=x_grouped[n][:, g].rearrange("p (c i) t -> p c t i", i=RUN),
-                in_=x_raw[n][:, g].rearrange("p t (c i) -> p c t i", i=RUN),
-            )
+            k = PASSES * n + g
+            if k < VECTOR_COPIES:
+                shares = ((nc.vector.tensor_copy, 0, PIXELS),)
+            elif k == SHARED_COPY:
+                shares = ((nc.vector.tensor_copy, 0, VECTOR_PIXELS), (nc.scalar.copy, VECTOR_PIXELS, PIXELS))
+            else:
+                shares = ((nc.scalar.copy, 0, PIXELS),)
+            for copy, first, end in shares:
+                copy(
+                    out=x_grouped[n][:, g, first:end].rearrange("p (c i) t -> p c t i", i=RUN),
+                    in_=x_raw[n][:, g, :, first:end].rearrange("p t (c i) -> p c t i", i=RUN),
+                )
 
         def quantise(n, passes=slice(0, PASSES)):
             nc.vector.quantize_mx(
@@ -167,7 +176,7 @@ def tile_axialshift_pa_kernel(tc, x, w1_words, w1_scales, b1, g1, be1, out):
             )
 
         products = {}
-        held = [keep.tile([P, PAIR, PIXELS], F32, name="held%d" % n) for n in range(HELD)]
+        held = {key: keep.tile([P, PAIR, PIXELS], F32, name="held%d_%d" % key) for key in HELD}
         stats = [keep.tile([P, GROUPS, 3], F32, name="stats%d" % n) for n in range(SAMPLES)]
         cross = [keep.tile([P, GROUPS], F32, name="cross%d" % n) for n in range(SAMPLES)]
         for n in range(SAMPLES):
@@ -234,11 +243,11 @@ def tile_axialshift_pa_kernel(tc, x, w1_words, w1_scales, b1, g1, be1, out):
                 out=moments[n][:, 2:3], in0=moments[n][:, 0:1], scalar1=-1.0, scalar2=None, op0=ALU.mult
             )
 
-        def hold(n):
-            nc.scalar.copy(out=held[n][:], in_=products[(n, 0)][:])
+        def hold(n, i):
+            nc.scalar.copy(out=held[(n, i)][:], in_=products[(n, i)][:])
 
         def sample_totals(n):
-            bank = BANKS * (n % 2) if n < HELD else BANKS * ((n + 1) % 2) + 1
+            bank = BANKS * (min(n, SAMPLES - 2) % 2)
             total = banks.tile([P, 4], F32, tag="bank%d" % bank, name="total%d" % n)
             totals[n] = total
             terms = (bias_terms[:, n, :], moments[n][:])
@@ -270,7 +279,7 @@ def tile_axialshift_pa_kernel(tc, x, w1_words, w1_scales, b1, g1, be1, out):
 
         def gelu_and_store(n, i, last):
             result = results.tile([P, PAIR, PIXELS], F32, name="result")
-            source = held[n] if i == 0 and n < HELD else products[(n, i)]
+            source = held.get((n, i), products[(n, i)])
             for jj in range(PAIR):
                 j = PAIR * i + jj
                 nc.scalar.activation(
@@ -290,6 +299,10 @@ def tile_axialshift_pa_kernel(tc, x, w1_words, w1_scales, b1, g1, be1, out):
                     in_=result[:],
                 )
 
+        def gelus_and_stores(n, order):
+            for i in order:
+                gelu_and_store(n, i, n == SAMPLES - 1 and i == BANKS - 1)
+
         warm_up(2, x_raw[0][:, 0].rearrange("p t w -> p (t w)")[:, 0 : 4 * P])
         for g in range(PASSES):
             regroup(0, g)
@@ -304,7 +317,7 @@ def tile_axialshift_pa_kernel(tc, x, w1_words, w1_scales, b1, g1, be1, out):
             multiply(0, i)
             statistics(0, i)
             if i == 0:
-                hold(0)
+                hold(0, 0)
                 regroup(2, 1)
                 for g in range(PASSES):
                     regroup(3, g)
@@ -314,31 +327,56 @@ def tile_axialshift_pa_kernel(tc, x, w1_words, w1_scales, b1, g1, be1, out):
                 prepare_params()
         square_bias()
         multiply(1, 0)
-        for n in range(SAMPLES):
-            following = n + 1
-            more = following < SAMPLES
-            partition_moments(n)
-            if more:
-                multiply(following, 1)
-            sample_totals(n)
-            if more:
-                multiply(following, 2)
-                statistics(following, 0)
-            if following < HELD:
-                quantise(following + 1)
-            variance(n)
-            if more:
-                multiply(following, 3)
-            if following < HELD:
-                hold(following)
-                multiply(following + 1, 0)
-            if more:
-                statistics(following, 1)
-                statistics(following, 2)
-            if following < HELD:
-                fill(following, 1)
-            coefficients(n)
-            for i in (1, 2, 3, 0) if n < HELD else range(BANKS):
-                gelu_and_store(n, i, n == SAMPLES - 1 and i == BANKS - 1)
-            if more:
-                statistics(following, 3)
+
+        partition_moments(0)
+        multiply(1, 1)
+        sample_totals(0)
+        multiply(1, 2)
+        statistics(1, 0)
+        quantise(2)
+        variance(0)
+        multiply(1, 3)
+        hold(1, 0)
+        multiply(2, 0)
+        statistics(1, 1)
+        statistics(1, 2)
+        fill(1, 2)
+        coefficients(0)
+        gelus_and_stores(0, (1, 2, 3, 0))
+        statistics(1, 3)
+
+        hold(1, 1)
+        partition_moments(1)
+        multiply(2, 1)
+        sample_totals(1)
+        multiply(2, 2)
+        statistics(2, 0)
+        quantise(3)
+        variance(1)
+        multiply(2, 3)
+        hold(2, 0)
+        multiply(3, 0)
+        multiply(3, 1)
+        statistics(2, 1)
+        statistics(2, 2)
+        coefficients(1)
+        gelus_and_stores(1, (2, 3, 0, 1))
+        statistics(2, 3)
+
+        partition_moments(2)
+        multiply(3, 2)
+        sample_totals(2)
+        statistics(3, 0)
+        statistics(3, 1)
+        variance(2)
+        multiply(3, 3)
+        statistics(3, 2)
+        statistics(3, 3)
+        coefficients(2)
+        gelus_and_stores(2, (1, 2, 3, 0))
+
+        partition_moments(3)
+        sample_totals(3)
+        variance(3)
+        coefficients(3)
+        gelus_and_stores(3, range(BANKS))

@@ -28,11 +28,11 @@ PAIR = 2
 BANKS = OUT_TILES // PAIR
 RUN = 4
 VECTOR_COPIES = 3
-GROUPS = OUT_TILES + 2
+GROUPS = OUT_TILES + 1
 TERMS = 3
 HELD = ((0, 0), (1, 0), (1, 1), (2, 0))
-SHARED_COPY = 3
-VECTOR_PIXELS = 96
+SHARED = {1: 160, 3: 96}
+QUARTER = PASSES * PIXELS // 4
 WARM_UP = 8
 
 FLOPS = 2 * SAMPLES * PIXELS * CHANNELS * CHANNELS
@@ -63,7 +63,6 @@ def tile_axialshift_pa_kernel(tc, x, w1_words, w1_scales, b1, g1, be1, out):
 
         nc.vector.memset(w_scales[:].bitcast(I32), 0)
         nc.vector.memset(warm_in[:], 0.0)
-        nc.vector.memset(zeros[:], 0.0)
         nc.vector.memset(param_rows[:], 0.0)
 
         load_x(0)
@@ -87,30 +86,41 @@ def tile_axialshift_pa_kernel(tc, x, w1_words, w1_scales, b1, g1, be1, out):
         average = keep.tile([P, P], F32)
         minus_half = keep.tile([P, 1], F32)
         make_identity(nc, identity[:])
+        nc.gpsimd.memset(zeros[:], 0.0)
         nc.gpsimd.memset(average[:], 1.0 / P)
         nc.gpsimd.memset(minus_half[:], -0.5)
 
-        select = keep.tile([P, 4 * OUT_TILES + SAMPLES * TERMS], BF16)
-        params = keep.tile([P, 4 * OUT_TILES + 2], F32)
-        bias = params[:, 0:OUT_TILES]
-        gain = params[:, OUT_TILES : 2 * OUT_TILES]
-        beta = params[:, 2 * OUT_TILES : 3 * OUT_TILES]
-        cross_weights = params[:, 3 * OUT_TILES : 4 * OUT_TILES + 2]
-        bias_terms = keep.tile([P, SAMPLES, TERMS], F32)
+        rows = {name: slice(r * OUT_TILES, (r + 1) * OUT_TILES) for r, name in enumerate(("bias", "gain", "beta"))}
+        gains_at = 2 * OUT_TILES
+        means_at = gains_at + SAMPLES * 2 * OUT_TILES
+        bias_at = means_at + 2
+        quarters_at = bias_at + OUT_TILES
+        linear = quarters_at + OUT_TILES
+        select = keep.tile([P, linear], BF16)
+        params = keep.tile([P, linear], F32)
+        zero_beta = params[:, 0 : 2 * OUT_TILES]
+        gain = params[:, gains_at : gains_at + OUT_TILES]
+        gain_centred = [params[:, gains_at + 2 * n * OUT_TILES : gains_at + 2 * (n + 1) * OUT_TILES] for n in range(SAMPLES)]
+        bias_means = params[:, means_at:bias_at]
+        bias = params[:, bias_at:quarters_at]
+        quarters = params[:, quarters_at:linear]
         bias_gain = keep.tile([P, OUT_TILES], F32)
         squares = keep.tile([P, OUT_TILES], F32)
-        nc.vector.memset(params[:, 4 * OUT_TILES + 1 :], EPS)
+        mean_square = keep.tile([P, 1], F32)
+        plus_minus = keep.tile([P, 2], F32)
+        nc.vector.memset(plus_minus[:, 0:1], 1.0)
+        nc.vector.memset(plus_minus[:, 1:2], -1.0)
         nc.vector.memset(select[:], 0.0)
-        bias_means = select[0:OUT_TILES, 4 * OUT_TILES :].rearrange("p (n c) -> p n c", c=TERMS)
-        nc.vector.memset(bias_means[:, :, 0], 1.0 / OUT_TILES)
-        nc.vector.memset(bias_means[:, :, 2], -1.0 / OUT_TILES)
-        nc.vector.tensor_copy(out=select[:, 0 : 3 * OUT_TILES], in_=identity[:, 0 : 3 * OUT_TILES])
+        nc.vector.memset(select[rows["bias"], means_at : means_at + 1], 1.0 / OUT_TILES)
+        nc.vector.memset(select[rows["bias"], means_at + 1 : bias_at], -1.0 / OUT_TILES)
+        nc.vector.tensor_copy(out=select[:, OUT_TILES : 2 * OUT_TILES], in_=identity[:, rows["beta"]])
+        nc.vector.tensor_copy(
+            out=select[:, gains_at:means_at].rearrange("p (n c j) -> p n c j", c=2, j=OUT_TILES)[:, :, 0],
+            in_=identity[:, rows["gain"]].unsqueeze(1).to_broadcast([P, SAMPLES, OUT_TILES]),
+        )
+        nc.vector.tensor_copy(out=select[:, bias_at:quarters_at], in_=identity[:, rows["bias"]])
         nc.vector.tensor_scalar(
-            out=select[:, 3 * OUT_TILES : 4 * OUT_TILES],
-            in0=identity[:, 0:OUT_TILES],
-            scalar1=0.25,
-            scalar2=None,
-            op0=ALU.mult,
+            out=select[:, quarters_at:linear], in0=identity[:, rows["bias"]], scalar1=0.25, scalar2=None, op0=ALU.mult
         )
         warmed = []
 
@@ -126,14 +136,8 @@ def tile_axialshift_pa_kernel(tc, x, w1_words, w1_scales, b1, g1, be1, out):
 
         def prepare_params():
             columns = banks.tile([P, 4 * P], F32, tag="bank7", name="param_columns")
-            linear = 4 * OUT_TILES
-            nc.tensor.matmul(
-                out=columns[:, 0 : linear + SAMPLES * TERMS], lhsT=param_rows[:], rhs=select[:], start=True, stop=True
-            )
+            nc.tensor.matmul(out=columns[:, 0:linear], lhsT=param_rows[:], rhs=select[:], start=True, stop=True)
             nc.vector.tensor_copy(out=params[:, 0:linear], in_=columns[:, 0:linear])
-            nc.vector.tensor_copy(
-                out=bias_terms[:].rearrange("p n c -> p (n c)"), in_=columns[:, linear : linear + SAMPLES * TERMS]
-            )
             nc.gpsimd.tensor_tensor(out=bias_gain[:], in0=bias, in1=gain, op=ALU.mult)
 
         def square_bias():
@@ -144,7 +148,7 @@ def tile_axialshift_pa_kernel(tc, x, w1_words, w1_scales, b1, g1, be1, out):
                 in1=bias,
                 op0=ALU.mult,
                 op1=ALU.mult,
-                accum_out=params[:, 4 * OUT_TILES : 4 * OUT_TILES + 1],
+                accum_out=mean_square[:],
             )
 
         x_grouped = [
@@ -156,10 +160,10 @@ def tile_axialshift_pa_kernel(tc, x, w1_words, w1_scales, b1, g1, be1, out):
 
         def regroup(n, g):
             k = PASSES * n + g
-            if k < VECTOR_COPIES:
+            if k in SHARED:
+                shares = ((nc.vector.tensor_copy, 0, SHARED[k]), (nc.scalar.copy, SHARED[k], PIXELS))
+            elif k < VECTOR_COPIES:
                 shares = ((nc.vector.tensor_copy, 0, PIXELS),)
-            elif k == SHARED_COPY:
-                shares = ((nc.vector.tensor_copy, 0, VECTOR_PIXELS), (nc.scalar.copy, VECTOR_PIXELS, PIXELS))
             else:
                 shares = ((nc.scalar.copy, 0, PIXELS),)
             for copy, first, end in shares:
@@ -168,26 +172,27 @@ def tile_axialshift_pa_kernel(tc, x, w1_words, w1_scales, b1, g1, be1, out):
                     in_=x_raw[n][:, g, :, first:end].rearrange("p t (c i) -> p c t i", i=RUN),
                 )
 
-        def quantise(n, passes=slice(0, PASSES)):
+        def quantise(n, first=0, end=PASSES * PIXELS):
             nc.vector.quantize_mx(
-                out=x_codes[n][:, passes].rearrange("p g w -> p (g w)").bitcast(FP8X4),
-                scales=x_scales[n][:, passes].rearrange("p g w -> p (g w)"),
-                in_=x_grouped[n][:, passes].rearrange("p g w t -> p (g w t)"),
+                out=x_codes[n][:].rearrange("p g w -> p (g w)")[:, first:end].bitcast(FP8X4),
+                scales=x_scales[n][:].rearrange("p g w -> p (g w)")[:, first:end],
+                in_=x_grouped[n][:].rearrange("p g w t -> p (g w t)")[:, PACK * first : PACK * end],
             )
 
         products = {}
         held = {key: keep.tile([P, PAIR, PIXELS], F32, name="held%d_%d" % key) for key in HELD}
-        stats = [keep.tile([P, GROUPS, 3], F32, name="stats%d" % n) for n in range(SAMPLES)]
-        cross = [keep.tile([P, GROUPS], F32, name="cross%d" % n) for n in range(SAMPLES)]
-        for n in range(SAMPLES):
-            nc.vector.memset(stats[n][:, OUT_TILES:, :], 1.0)
-        moments = [keep.tile([P, 3], F32, name="moments%d" % n) for n in range(SAMPLES)]
+        stats = keep.tile([P, SAMPLES, GROUPS, 3], F32)
+        nc.vector.memset(stats[:, :, OUT_TILES, :], 1.0)
+        weights = keep.tile([P, SAMPLES, GROUPS, 2], F32)
+        nc.vector.memset(weights[:, :, 0:OUT_TILES, 1], 1.0 / (OUT_TILES * PIXELS))
+        nc.vector.memset(weights[:, :, OUT_TILES, 1], EPS)
+        terms = [keep.tile([P, GROUPS, 2], F32, name="terms%d" % n) for n in range(SAMPLES)]
+        spread = [keep.tile([P, 2], F32, name="spread%d" % n) for n in range(SAMPLES)]
+        moments = [keep.tile([P, TERMS], F32, name="moments%d" % n) for n in range(SAMPLES)]
         totals = {}
         var_eps = [keep.tile([P, 1], F32, name="var_eps%d" % n) for n in range(SAMPLES)]
         rstd = [keep.tile([P, 1], F32, name="rstd%d" % n) for n in range(SAMPLES)]
-        centred = [keep.tile([P, OUT_TILES], F32, name="centred%d" % n) for n in range(SAMPLES)]
-        scale = [keep.tile([P, OUT_TILES], F32, name="scale%d" % n) for n in range(SAMPLES)]
-        shift = [keep.tile([P, OUT_TILES], F32, name="shift%d" % n) for n in range(SAMPLES)]
+        scale_shift = [keep.tile([P, 2, OUT_TILES], F32, name="scale_shift%d" % n) for n in range(SAMPLES)]
 
         def multiply(n, i):
             products[(n, i)] = banks.tile(
@@ -214,33 +219,41 @@ def tile_axialshift_pa_kernel(tc, x, w1_words, w1_scales, b1, g1, be1, out):
 
         def statistics(n, i):
             nc.vector.bn_stats(
-                out=stats[n][:, PAIR * i : PAIR * (i + 1), :].rearrange("p j s -> p (j s)"),
+                out=stats[:, n, PAIR * i : PAIR * (i + 1), :].rearrange("p j s -> p (j s)"),
                 in_=products[(n, i)][:].rearrange("p j w -> p w j"),
             )
 
         def partition_moments(n):
-            nc.vector.bn_aggr(
-                out=moments[n][:, 0:2], in_=stats[n][:, 0:OUT_TILES].rearrange("p j s -> p (j s)")
-            )
+            if n == 0:
+                quantise(2, 0, QUARTER)
             nc.vector.scalar_tensor_tensor(
-                out=cross[n][:],
-                in0=stats[n][:, :, 1],
-                scalar=1.0,
-                in1=cross_weights,
-                op0=ALU.mult,
-                op1=ALU.mult,
-                accum_out=bias_terms[:, n, 1:2],
-            )
-            nc.vector.scalar_tensor_tensor(
-                out=moments[n][:, 1:2],
-                in0=moments[n][:, 0:1],
-                scalar=moments[n][:, 0:1],
-                in1=moments[n][:, 1:2],
+                out=weights[:, n, 0:OUT_TILES, 0],
+                in0=stats[:, n, 0:OUT_TILES, 1],
+                scalar=1.0 / OUT_TILES,
+                in1=quarters,
                 op0=ALU.mult,
                 op1=ALU.add,
             )
-            nc.vector.tensor_scalar(
-                out=moments[n][:, 2:3], in0=moments[n][:, 0:1], scalar1=-1.0, scalar2=None, op0=ALU.mult
+            nc.vector.bn_aggr(out=spread[n][:], in_=stats[:, n, 0:OUT_TILES].rearrange("p j s -> p (j s)"))
+            if n == 0:
+                nc.vector.tensor_copy(out=weights[:, :, OUT_TILES, 0], in_=mean_square[:].to_broadcast([P, SAMPLES]))
+                quantise(2, QUARTER, 2 * QUARTER)
+            nc.vector.scalar_tensor_tensor(
+                out=terms[n][:],
+                in0=stats[:, n, :, 1:3],
+                scalar=1.0,
+                in1=weights[:, n],
+                op0=ALU.mult,
+                op1=ALU.mult,
+                accum_out=moments[n][:, 0:1],
+            )
+            nc.vector.scalar_tensor_tensor(
+                out=moments[n][:, 1:3],
+                in0=plus_minus[:],
+                scalar=spread[n][:, 0:1],
+                in1=bias_means,
+                op0=ALU.mult,
+                op1=ALU.add,
             )
 
         def hold(n, i):
@@ -250,31 +263,31 @@ def tile_axialshift_pa_kernel(tc, x, w1_words, w1_scales, b1, g1, be1, out):
             bank = BANKS * (min(n, SAMPLES - 2) % 2)
             total = banks.tile([P, 4], F32, tag="bank%d" % bank, name="total%d" % n)
             totals[n] = total
-            terms = (bias_terms[:, n, :], moments[n][:])
-            for k, term in enumerate(terms):
-                nc.tensor.matmul(
-                    out=total[:, 0:TERMS], lhsT=average[:], rhs=term, start=(k == 0), stop=(k == len(terms) - 1)
-                )
+            nc.tensor.matmul(out=total[:, 0:TERMS], lhsT=average[:], rhs=moments[n][:], start=True, stop=True)
 
         def variance(n):
             total = totals[n]
             nc.vector.tensor_scalar(
                 out=var_eps[n][:],
-                in0=total[:, 0:1],
+                in0=total[:, 1:2],
                 scalar1=total[:, 2:3],
-                scalar2=total[:, 1:2],
+                scalar2=total[:, 0:1],
                 op0=ALU.mult,
                 op1=ALU.add,
             )
             nc.vector.scalar_tensor_tensor(
-                out=centred[n][:], in0=gain, scalar=total[:, 2:3], in1=bias_gain[:], op0=ALU.mult, op1=ALU.add
+                out=gain_centred[n][:, OUT_TILES:], in0=gain, scalar=total[:, 2:3], in1=bias_gain[:], op0=ALU.mult, op1=ALU.add
             )
             nc.gpsimd.tensor_tensor(out=rstd[n][:], in0=var_eps[n][:], in1=minus_half[:], op=ALU.pow)
 
         def coefficients(n):
-            nc.vector.tensor_scalar(out=scale[n][:], in0=gain, scalar1=rstd[n][:], scalar2=None, op0=ALU.mult)
             nc.vector.scalar_tensor_tensor(
-                out=shift[n][:], in0=centred[n][:], scalar=rstd[n][:], in1=beta, op0=ALU.mult, op1=ALU.add
+                out=scale_shift[n][:].rearrange("p c j -> p (c j)"),
+                in0=gain_centred[n],
+                scalar=rstd[n][:],
+                in1=zero_beta,
+                op0=ALU.mult,
+                op1=ALU.add,
             )
 
         def gelu_and_store(n, i, last):
@@ -286,8 +299,8 @@ def tile_axialshift_pa_kernel(tc, x, w1_words, w1_scales, b1, g1, be1, out):
                     out=result[:, jj, :],
                     in_=source[:, jj, :],
                     func=ACT.Gelu,
-                    scale=scale[n][:, j : j + 1],
-                    bias=shift[n][:, j : j + 1],
+                    scale=scale_shift[n][:, 0, j : j + 1],
+                    bias=scale_shift[n][:, 1, j : j + 1],
                 )
                 if last:
                     nc.sync.dma_start(
@@ -308,9 +321,8 @@ def tile_axialshift_pa_kernel(tc, x, w1_words, w1_scales, b1, g1, be1, out):
             regroup(0, g)
         warm_up(2, x_grouped[0][:, 1].rearrange("p w t -> p (w t)")[:, 0 : 4 * P])
         for g in range(PASSES):
-            quantise(0, slice(g, g + 1))
+            quantise(0, g * PIXELS, (g + 1) * PIXELS)
         regroup(1, 0)
-        quantise(1, slice(0, 1))
         regroup(1, 1)
         regroup(2, 0)
         for i in range(BANKS):
@@ -322,7 +334,7 @@ def tile_axialshift_pa_kernel(tc, x, w1_words, w1_scales, b1, g1, be1, out):
                 for g in range(PASSES):
                     regroup(3, g)
             if i == 1:
-                quantise(1, slice(1, 2))
+                quantise(1)
             if i == 2:
                 prepare_params()
         square_bias()
@@ -333,7 +345,7 @@ def tile_axialshift_pa_kernel(tc, x, w1_words, w1_scales, b1, g1, be1, out):
         sample_totals(0)
         multiply(1, 2)
         statistics(1, 0)
-        quantise(2)
+        quantise(2, 2 * QUARTER)
         variance(0)
         multiply(1, 3)
         hold(1, 0)

@@ -31,7 +31,9 @@ VECTOR_COPIES = 3
 GROUPS = OUT_TILES + 1
 TERMS = 3
 HELD = ((0, 0), (1, 0), (1, 1), (2, 0))
-SHARED = {1: 160, 3: 96}
+SHARED = {1: 160, 2: 128, 3: 64}
+GPSIMD_COPY = 7
+GPSIMD_PIXELS = 160
 QUARTER = PASSES * PIXELS // 4
 WARM_UP = 8
 
@@ -158,12 +160,17 @@ def tile_axialshift_pa_kernel(tc, x, w1_words, w1_scales, b1, g1, be1, out):
         x_codes = [keep.tile([P, PASSES, PIXELS], U32, name="x_codes%d" % n, align_bytes=64) for n in range(SAMPLES)]
         x_scales = [keep.tile([P, PASSES, PIXELS], U8, name="x_scales%d" % n, align_bytes=64) for n in range(SAMPLES)]
 
+        def gpsimd_copy(out, in_):
+            nc.gpsimd.tensor_scalar(out=out, in0=in_, scalar1=1.0, scalar2=0.0, op0=ALU.mult, op1=ALU.add)
+
         def regroup(n, g):
             k = PASSES * n + g
             if k in SHARED:
                 shares = ((nc.vector.tensor_copy, 0, SHARED[k]), (nc.scalar.copy, SHARED[k], PIXELS))
             elif k < VECTOR_COPIES:
                 shares = ((nc.vector.tensor_copy, 0, PIXELS),)
+            elif k == GPSIMD_COPY:
+                shares = ((nc.scalar.copy, 0, GPSIMD_PIXELS), (gpsimd_copy, GPSIMD_PIXELS, PIXELS))
             else:
                 shares = ((nc.scalar.copy, 0, PIXELS),)
             for copy, first, end in shares:

from contextlib import ExitStack

import concourse.mybir as mybir
from concourse.masks import make_identity

F32 = mybir.dt.float32
BF16 = mybir.dt.bfloat16
U8 = mybir.dt.uint8
U32 = mybir.dt.uint32
I32 = mybir.dt.int32
FP8X4 = mybir.dt.float8_e4m3fn_x4
FP4X4 = mybir.dt.float4_e2m1fn_x4
ALU = mybir.AluOpType
ACT = mybir.ActivationFunctionType

SAMPLES = 4
CHANNELS = 1024
PIXELS = 256
EPS = 1e-5

P = 128
PACK = 4
K_PASS = P * PACK
PASSES = CHANNELS // K_PASS
OUT_TILES = CHANNELS // P
COLS = 128
PAIR = 2
BANKS = OUT_TILES // PAIR
RUN = 4
VECTOR_COPIES = 3
GROUPS = OUT_TILES + 1
TERMS = 3
HELD = ((0, 0), (1, 0), (1, 1), (2, 0))
SHARED = {1: 160, 2: 128, 3: 64}
GPSIMD_COPY = 7
GPSIMD_PIXELS = 160
QUARTER = PASSES * PIXELS // 4
WARM_UP = 8

FLOPS = 2 * SAMPLES * PIXELS * CHANNELS * CHANNELS


def tile_axialshift_pa_kernel(tc, x, w1_words, w1_scales, b1, g1, be1, out):
    nc = tc.nc
    with ExitStack() as ctx:
        keep = ctx.enter_context(tc.tile_pool(name="keep", bufs=1))
        results = ctx.enter_context(tc.tile_pool(name="results", bufs=8))
        banks = ctx.enter_context(tc.psum_pool(name="banks", bufs=1))
        ctx.enter_context(tc.manual_schedule())

        x_raw = [keep.tile([P, PASSES, PACK, PIXELS], BF16, name="x_raw%d" % n) for n in range(SAMPLES)]
        w_words = keep.tile([P, PASSES, 2 * CHANNELS], U8, align_bytes=64)
        w_scales = keep.tile([P, PASSES, CHANNELS], U8, align_bytes=64)
        param_rows = keep.tile([P, P], BF16)
        warm_in = keep.tile([P, 1], F32)
        warm_out = keep.tile([P, 1], F32)
        zeros = keep.tile([P, 4 * P], BF16)

        def load_x(n):
            for g in range(PASSES):
                nc.sync.dma_start(
                    out=x_raw[n][:, g],
                    in_=x[n, g * K_PASS : (g + 1) * K_PASS].rearrange("(p t) h w -> p t (h w)", t=PACK),
                )

        nc.vector.memset(w_scales[:].bitcast(I32), 0)
        nc.vector.memset(warm_in[:], 0.0)
        nc.vector.memset(param_rows[:], 0.0)

        load_x(0)
        for r in range(4):
            nc.sync.dma_start(
                out=w_scales[r:P:32].bitcast(I32),
                in_=w1_scales[:, r:16:4, :].rearrange("g q n -> q g n").bitcast(I32),
            )
        nc.sync.dma_start(out=w_words[:].bitcast(I32), in_=w1_words.rearrange("g p b -> p g b").bitcast(I32))
        load_x(1)
        nc.scalar.activation(out=warm_out[:], in_=warm_in[:], func=ACT.Gelu)
        for r, vector in enumerate((b1, g1, be1)):
            nc.sync.dma_start(
                out=param_rows[r * OUT_TILES : (r + 1) * OUT_TILES, :],
                in_=vector.rearrange("(j p) -> j p", p=P),
            )
        for n in range(2, SAMPLES):
            load_x(n)

        identity = keep.tile([P, P], BF16)
        average = keep.tile([P, P], F32)
        minus_half = keep.tile([P, 1], F32)
        make_identity(nc, identity[:])
        nc.gpsimd.memset(zeros[:], 0.0)
        nc.gpsimd.memset(average[:], 1.0 / P)
        nc.gpsimd.memset(minus_half[:], -0.5)

        rows = {name: slice(r * OUT_TILES, (r + 1) * OUT_TILES) for r, name in enumerate(("bias", "gain", "beta"))}
        gains_at = 2 * OUT_TILES
        means_at = gains_at + SAMPLES * 2 * OUT_TILES
        bias_at = means_at + 2
        quarters_at = bias_at + OUT_TILES
        linear = quarters_at + OUT_TILES
        select = keep.tile([P, linear], BF16)
        params = keep.tile([P, linear], F32)
        zero_beta = params[:, 0 : 2 * OUT_TILES]
        gain = params[:, gains_at : gains_at + OUT_TILES]
        gain_centred = [params[:, gains_at + 2 * n * OUT_TILES : gains_at + 2 * (n + 1) * OUT_TILES] for n in range(SAMPLES)]
        bias_means = params[:, means_at:bias_at]
        bias = params[:, bias_at:quarters_at]
        quarters = params[:, quarters_at:linear]
        bias_gain = keep.tile([P, OUT_TILES], F32)
        squares = keep.tile([P, OUT_TILES], F32)
        mean_square = keep.tile([P, 1], F32)
        plus_minus = keep.tile([P, 2], F32)
        nc.vector.memset(plus_minus[:, 0:1], 1.0)
        nc.vector.memset(plus_minus[:, 1:2], -1.0)
        nc.vector.memset(select[:], 0.0)
        nc.vector.memset(select[rows["bias"], means_at : means_at + 1], 1.0 / OUT_TILES)
        nc.vector.memset(select[rows["bias"], means_at + 1 : bias_at], -1.0 / OUT_TILES)
        nc.vector.tensor_copy(out=select[:, OUT_TILES : 2 * OUT_TILES], in_=identity[:, rows["beta"]])
        nc.vector.tensor_copy(
            out=select[:, gains_at:means_at].rearrange("p (n c j) -> p n c j", c=2, j=OUT_TILES)[:, :, 0],
            in_=identity[:, rows["gain"]].unsqueeze(1).to_broadcast([P, SAMPLES, OUT_TILES]),
        )
        nc.vector.tensor_copy(out=select[:, bias_at:quarters_at], in_=identity[:, rows["bias"]])
        nc.vector.tensor_scalar(
            out=select[:, quarters_at:linear], in0=identity[:, rows["bias"]], scalar1=0.25, scalar2=None, op0=ALU.mult
        )
        warmed = []

        def warm_up(count, moving):
            for k in range(count):
                scratch = banks.tile(
                    [P, 4 * P], F32, tag="bank%d" % (BANKS + len(warmed) % 3), name="scratch%d" % len(warmed)
                )
                warmed.append(scratch)
                nc.tensor.matmul(out=scratch[:], lhsT=identity[:], rhs=moving, start=True, stop=True)

        warm_up(WARM_UP - 4, zeros[:])

        def prepare_params():
            columns = banks.tile([P, 4 * P], F32, tag="bank7", name="param_columns")
            nc.tensor.matmul(out=columns[:, 0:linear], lhsT=param_rows[:], rhs=select[:], start=True, stop=True)
            nc.vector.tensor_copy(out=params[:, 0:linear], in_=columns[:, 0:linear])
            nc.gpsimd.tensor_tensor(out=bias_gain[:], in0=bias, in1=gain, op=ALU.mult)

        def square_bias():
            nc.vector.scalar_tensor_tensor(
                out=squares[:],
                in0=bias,
                scalar=1.0 / OUT_TILES,
                in1=bias,
                op0=ALU.mult,
                op1=ALU.mult,
                accum_out=mean_square[:],
            )

        x_grouped = [
            keep.tile([P, PASSES, PIXELS, PACK], BF16, name="x_grouped%d" % n, align_bytes=64)
            for n in range(SAMPLES)
        ]
        x_codes = [keep.tile([P, PASSES, PIXELS], U32, name="x_codes%d" % n, align_bytes=64) for n in range(SAMPLES)]
        x_scales = [keep.tile([P, PASSES, PIXELS], U8, name="x_scales%d" % n, align_bytes=64) for n in range(SAMPLES)]

        def gpsimd_copy(out, in_):
            nc.gpsimd.tensor_scalar(out=out, in0=in_, scalar1=1.0, scalar2=0.0, op0=ALU.mult, op1=ALU.add)

        def regroup(n, g):
            k = PASSES * n + g
            if k in SHARED:
                shares = ((nc.vector.tensor_copy, 0, SHARED[k]), (nc.scalar.copy, SHARED[k], PIXELS))
            elif k < VECTOR_COPIES:
                shares = ((nc.vector.tensor_copy, 0, PIXELS),)
            elif k == GPSIMD_COPY:
                shares = ((nc.scalar.copy, 0, GPSIMD_PIXELS), (gpsimd_copy, GPSIMD_PIXELS, PIXELS))
            else:
                shares = ((nc.scalar.copy, 0, PIXELS),)
            for copy, first, end in shares:
                copy(
                    out=x_grouped[n][:, g, first:end].rearrange("p (c i) t -> p c t i", i=RUN),
                    in_=x_raw[n][:, g, :, first:end].rearrange("p t (c i) -> p c t i", i=RUN),
                )

        def quantise(n, first=0, end=PASSES * PIXELS):
            nc.vector.quantize_mx(
                out=x_codes[n][:].rearrange("p g w -> p (g w)")[:, first:end].bitcast(FP8X4),
                scales=x_scales[n][:].rearrange("p g w -> p (g w)")[:, first:end],
                in_=x_grouped[n][:].rearrange("p g w t -> p (g w t)")[:, PACK * first : PACK * end],
            )

        products = {}
        held = {key: keep.tile([P, PAIR, PIXELS], F32, name="held%d_%d" % key) for key in HELD}
        stats = keep.tile([P, SAMPLES, GROUPS, 3], F32)
        nc.vector.memset(stats[:, :, OUT_TILES, :], 1.0)
        weights = keep.tile([P, SAMPLES, GROUPS, 2], F32)
        nc.vector.memset(weights[:, :, 0:OUT_TILES, 1], 1.0 / (OUT_TILES * PIXELS))
        nc.vector.memset(weights[:, :, OUT_TILES, 1], EPS)
        terms = [keep.tile([P, GROUPS, 2], F32, name="terms%d" % n) for n in range(SAMPLES)]
        spread = [keep.tile([P, 2], F32, name="spread%d" % n) for n in range(SAMPLES)]
        moments = [keep.tile([P, TERMS], F32, name="moments%d" % n) for n in range(SAMPLES)]
        totals = {}
        var_eps = [keep.tile([P, 1], F32, name="var_eps%d" % n) for n in range(SAMPLES)]
        rstd = [keep.tile([P, 1], F32, name="rstd%d" % n) for n in range(SAMPLES)]
        scale_shift = [keep.tile([P, 2, OUT_TILES], F32, name="scale_shift%d" % n) for n in range(SAMPLES)]

        def multiply(n, i):
            products[(n, i)] = banks.tile(
                [P, PAIR, PIXELS], F32, tag="bank%d" % (BANKS * (n % 2) + i), name="product%d_%d" % (n, i)
            )
            fill(n, i)

        def fill(n, i):
            product = products[(n, i)]
            for jj in range(PAIR):
                j = PAIR * i + jj
                for h in range(PIXELS // COLS):
                    cols = slice(h * COLS, (h + 1) * COLS)
                    for g in range(PASSES):
                        nc.tensor.matmul_mx(
                            out=product[:, jj, cols],
                            lhsT=w_words[:, g, 2 * P * j : 2 * P * (j + 1)].bitcast(FP4X4),
                            lhsT_scale=w_scales[:, g, P * j : P * (j + 1)],
                            rhs=x_codes[n][:, g, cols].bitcast(FP8X4),
                            rhs_scale=x_scales[n][:, g, cols],
                            start=(g == 0),
                            stop=(g == PASSES - 1),
                        )

        def statistics(n, i):
            nc.vector.bn_stats(
                out=stats[:, n, PAIR * i : PAIR * (i + 1), :].rearrange("p j s -> p (j s)"),
                in_=products[(n, i)][:].rearrange("p j w -> p w j"),
            )

        def partition_moments(n):
            if n == 0:
                quantise(2, 0, QUARTER)
            nc.vector.scalar_tensor_tensor(
                out=weights[:, n, 0:OUT_TILES, 0],
                in0=stats[:, n, 0:OUT_TILES, 1],
                scalar=1.0 / OUT_TILES,
                in1=quarters,
                op0=ALU.mult,
                op1=ALU.add,
            )
            nc.vector.bn_aggr(out=spread[n][:], in_=stats[:, n, 0:OUT_TILES].rearrange("p j s -> p (j s)"))
            if n == 0:
                nc.vector.tensor_copy(out=weights[:, :, OUT_TILES, 0], in_=mean_square[:].to_broadcast([P, SAMPLES]))
                quantise(2, QUARTER, 2 * QUARTER)
            nc.vector.scalar_tensor_tensor(
                out=terms[n][:],
                in0=stats[:, n, :, 1:3],
                scalar=1.0,
                in1=weights[:, n],
                op0=ALU.mult,
                op1=ALU.mult,
                accum_out=moments[n][:, 0:1],
            )
            nc.vector.scalar_tensor_tensor(
                out=moments[n][:, 1:3],
                in0=plus_minus[:],
                scalar=spread[n][:, 0:1],
                in1=bias_means,
                op0=ALU.mult,
                op1=ALU.add,
            )

        def hold(n, i):
            nc.scalar.copy(out=held[(n, i)][:], in_=products[(n, i)][:])

        def sample_totals(n):
            bank = BANKS * (min(n, SAMPLES - 2) % 2)
            total = banks.tile([P, 4], F32, tag="bank%d" % bank, name="total%d" % n)
            totals[n] = total
            nc.tensor.matmul(out=total[:, 0:TERMS], lhsT=average[:], rhs=moments[n][:], start=True, stop=True)

        def variance(n):
            total = totals[n]
            nc.vector.tensor_scalar(
                out=var_eps[n][:],
                in0=total[:, 1:2],
                scalar1=total[:, 2:3],
                scalar2=total[:, 0:1],
                op0=ALU.mult,
                op1=ALU.add,
            )
            nc.vector.scalar_tensor_tensor(
                out=gain_centred[n][:, OUT_TILES:], in0=gain, scalar=total[:, 2:3], in1=bias_gain[:], op0=ALU.mult, op1=ALU.add
            )
            nc.gpsimd.tensor_tensor(out=rstd[n][:], in0=var_eps[n][:], in1=minus_half[:], op=ALU.pow)

        def coefficients(n):
            nc.vector.scalar_tensor_tensor(
                out=scale_shift[n][:].rearrange("p c j -> p (c j)"),
                in0=gain_centred[n],
                scalar=rstd[n][:],
                in1=zero_beta,
                op0=ALU.mult,
                op1=ALU.add,
            )

        def gelu_and_store(n, i, last):
            result = results.tile([P, PAIR, PIXELS], F32, name="result")
            source = held.get((n, i), products[(n, i)])
            for jj in range(PAIR):
                j = PAIR * i + jj
                nc.scalar.activation(
                    out=result[:, jj, :],
                    in_=source[:, jj, :],
                    func=ACT.Gelu,
                    scale=scale_shift[n][:, 0, j : j + 1],
                    bias=scale_shift[n][:, 1, j : j + 1],
                )
                if last:
                    nc.sync.dma_start(
                        out=out[n, j * P : (j + 1) * P].rearrange("p h w -> p (h w)"), in_=result[:, jj, :]
                    )
            if not last:
                nc.sync.dma_start(
                    out=out[n, PAIR * i * P : PAIR * (i + 1) * P].rearrange("(j p) h w -> p j (h w)", p=P),
                    in_=result[:],
                )

        def gelus_and_stores(n, order):
            for i in order:
                gelu_and_store(n, i, n == SAMPLES - 1 and i == BANKS - 1)

        warm_up(2, x_raw[0][:, 0].rearrange("p t w -> p (t w)")[:, 0 : 4 * P])
        for g in range(PASSES):
            regroup(0, g)
        warm_up(2, x_grouped[0][:, 1].rearrange("p w t -> p (w t)")[:, 0 : 4 * P])
        for g in range(PASSES):
            quantise(0, g * PIXELS, (g + 1) * PIXELS)
        regroup(1, 0)
        regroup(1, 1)
        regroup(2, 0)
        for i in range(BANKS):
            multiply(0, i)
            statistics(0, i)
            if i == 0:
                hold(0, 0)
                regroup(2, 1)
                for g in range(PASSES):
                    regroup(3, g)
            if i == 1:
                quantise(1)
            if i == 2:
                prepare_params()
        square_bias()
        multiply(1, 0)

        partition_moments(0)
        multiply(1, 1)
        sample_totals(0)
        multiply(1, 2)
        statistics(1, 0)
        quantise(2, 2 * QUARTER)
        variance(0)
        multiply(1, 3)
        hold(1, 0)
        multiply(2, 0)
        statistics(1, 1)
        statistics(1, 2)
        fill(1, 2)
        coefficients(0)
        gelus_and_stores(0, (1, 2, 3, 0))
        statistics(1, 3)

        hold(1, 1)
        partition_moments(1)
        multiply(2, 1)
        sample_totals(1)
        multiply(2, 2)
        statistics(2, 0)
        quantise(3)
        variance(1)
        multiply(2, 3)
        hold(2, 0)
        multiply(3, 0)
        multiply(3, 1)
        statistics(2, 1)
        statistics(2, 2)
        coefficients(1)
        gelus_and_stores(1, (2, 3, 0, 1))
        statistics(2, 3)

        partition_moments(2)
        multiply(3, 2)
        sample_totals(2)
        statistics(3, 0)
        statistics(3, 1)
        variance(2)
        multiply(3, 3)
        statistics(3, 2)
        statistics(3, 3)
        coefficients(2)
        gelus_and_stores(2, (1, 2, 3, 0))

        partition_moments(3)
        sample_totals(3)
        variance(3)
        coefficients(3)
        gelus_and_stores(3, range(BANKS))
